import numpy as np
import ml_dtypes


def mxq(x, axis, fmt="e4m3"):
    dtype, down = {"e4m3": (ml_dtypes.float8_e4m3fn, 7), "e5m2": (ml_dtypes.float8_e5m2, 14)}[fmt]
    v = np.moveaxis(np.asarray(x, np.float32).astype(ml_dtypes.bfloat16).astype(np.float64), axis, -1)
    blocks = v.reshape(v.shape[:-1] + (-1, 32))
    amax = np.abs(blocks).max(-1, keepdims=True)
    byte = np.maximum(np.where(amax > 0, np.frexp(amax)[1] - 1 + 127, 0) - down, 1)
    scale = np.exp2(byte - 127.0)
    codes = (blocks / scale).astype(np.float32).astype(dtype).astype(np.float64)
    return np.moveaxis((codes * scale).reshape(v.shape), -1, axis)


WIDE = False


def mx_kscale(k):
    if not WIDE:
        return np.ones(k)
    levels = np.array([10, -10, 5, -5, 0])
    a = np.random.permutation(np.resize(levels, k // 512 * 4)).reshape(k // 512, 4)
    idx = np.arange(k)
    return np.exp2(a[idx // 512, idx % 128 // 32])


BF16 = ml_dtypes.bfloat16


def bf(x):
    return np.asarray(x, np.float32).astype(BF16)


def f64(x):
    return np.asarray(x).astype(np.float64)


E2M1 = np.array([0.0, 0.5, 1.0, 1.5, 2.0, 3.0, 4.0, 6.0, -0.0, -0.5, -1.0, -1.5, -2.0, -3.0, -4.0, -6.0])


def pack_weight(w, fmt):
    k, n = w.shape
    w = f64(bf(w)).reshape(k // 32, 32, n)
    amax = np.abs(w).max(1)
    if fmt == "e4m3":
        byte = np.frexp(amax)[1] - 1 + 127 - 7
    else:
        mant, ex = np.frexp(amax / 6.0)
        byte = np.where(mant > 0.5, ex, ex - 1) + 127
    byte = np.clip(np.where(amax > 0, byte, 1), 1, 254)
    scaled = (w * np.exp2(127.0 - byte)[:, None, :]).reshape(k, n).astype(np.float32)
    by_word = np.ascontiguousarray(scaled.reshape(k // 512, 128, 4, n).transpose(0, 1, 3, 2))
    if fmt == "e4m3":
        words = by_word.astype(ml_dtypes.float8_e4m3fn).view(np.uint8)
    else:
        c = by_word.astype(ml_dtypes.float4_e2m1fn).view(np.uint8) & 0xF
        words = c[..., 0::2] | (c[..., 1::2] << 4)
    return np.ascontiguousarray(words), np.ascontiguousarray(byte.astype(np.uint8).reshape(k // 512, 16, n))


def unpack_weight(words, scales, fmt):
    g, p, n, _ = words.shape
    if fmt == "e4m3":
        vals = np.ascontiguousarray(words).view(ml_dtypes.float8_e4m3fn).astype(np.float64)
    else:
        nib = np.empty((g, p, n, 4), np.uint8)
        nib[..., 0::2] = words & 0xF
        nib[..., 1::2] = words >> 4
        vals = E2M1[nib]
    vals = vals * np.repeat(np.exp2(scales.astype(np.float64) - 127.0), 8, axis=1)[..., None]
    return vals.transpose(0, 1, 3, 2).reshape(g * 512, n)

def pack4(w):
    words, scales = pack_weight(w, "e2m1")
    return words.reshape(words.shape[0], 128, -1), scales


def unpack4(words, scales):
    return unpack_weight(words.reshape(words.shape[0], 128, -1, 2), scales, "e2m1")


B, D, H = 640, 1024, 1024
G = 4
QH = H % 512 == 0


def sigmoid(v):
    return 1.0 / (1.0 + np.exp(-v))


def setup_inputs():
    s = mx_kscale(D)
    t = mx_kscale(H) if QH else np.ones(H)
    x_t = bf(np.random.standard_normal((B, D)) * s)
    h_pre = bf(np.random.standard_normal((B, H)) * t)
    c_pre = bf(np.random.standard_normal((B, H)))
    Wx = np.random.standard_normal((G, H, D)) * 0.64 / np.sqrt(D) / s
    Wx_cat = np.ascontiguousarray(Wx.swapaxes(1, 2)).reshape(-1, H)
    Wx_words, Wx_scales = pack4(Wx_cat)
    bW = bf(np.random.standard_normal((4, H)) * 0.3)
    Uh = bf(np.random.standard_normal((4, H, H)) * 0.64 / np.sqrt(H) / t)
    bU = bf(np.random.standard_normal((4, H)) * 0.3)
    return {
        "x_t": x_t,
        "h_pre": h_pre,
        "c_pre": c_pre,
        "Wx_words": Wx_words,
        "Wx_scales": Wx_scales,
        "bW": bW,
        "Uh": Uh,
        "bU": bU,
    }


def reference(x_t, h_pre, c_pre, Wx_words, Wx_scales, bW, Uh, bU):
    zx = mxq(f64(x_t), 1, "e4m3") @ unpack4(Wx_words, Wx_scales).reshape(G, D, H)
    if QH:
        zh = mxq(f64(h_pre), 1, "e4m3") @ mxq(f64(Uh), 2, "e4m3").transpose(0, 2, 1)
    else:
        zh = f64(h_pre) @ f64(Uh).transpose(0, 2, 1)
    z = zx + zh + (f64(bW) + f64(bU))[:, None, :]
    f_t = sigmoid(z[0])
    i_t = sigmoid(z[1])
    o_t = sigmoid(z[2])
    g_t = np.tanh(z[3])
    c_t = f_t * f64(c_pre) + i_t * g_t
    h_t = o_t * np.tanh(c_t)
    return (h_t, c_t)

@@ -1,0 +1,271 @@
+from contextlib import ExitStack
+
+import concourse.mybir as mybir
+from concourse.masks import make_identity
+
+F32 = mybir.dt.float32
+BF16 = mybir.dt.bfloat16
+I32 = mybir.dt.int32
+U32 = mybir.dt.uint32
+U8 = mybir.dt.uint8
+FP8X4 = mybir.dt.float8_e4m3fn_x4
+FP4X4 = mybir.dt.float4_e2m1fn_x4
+ACT = mybir.ActivationFunctionType
+ALU = mybir.AluOpType
+
+P = 128
+BATCH = 640
+FEATURES = 1024
+GATES = 4
+GATE_F = 0
+GATE_I = 1
+GATE_O = 2
+GATE_G = 3
+K_PASS = 512
+PASSES = FEATURES // K_PASS
+N_TILE = 512
+HALVES = FEATURES // N_TILE
+BATCH_TILES = BATCH // P
+ROW_TILES = N_TILE // P
+WORDS = FEATURES // 2
+
+GATE_ORDER = (GATE_I, GATE_G, GATE_F, GATE_O)
+CHUNKS = HALVES * GATES
+STEPS = CHUNKS * BATCH_TILES
+
+UH_RAW_BUFS = 4
+TRANSPOSE_AT = 1
+QUANTISE_AT = 3
+
+FLOPS = 2 * BATCH * (2 * FEATURES) * (GATES * FEATURES)
+
+
+def tile_lstmcell_e_kernel(tc, x_t, h_pre, c_pre, Wx_words, Wx_scales, bW, Uh, bU, out_0, out_1):
+    nc = tc.nc
+    with ExitStack() as ctx:
+        keep = ctx.enter_context(tc.tile_pool(name="keep", bufs=1))
+        stage = ctx.enter_context(tc.tile_pool(name="stage", bufs=3))
+        uh_raw_pool = ctx.enter_context(tc.tile_pool(name="uh_raw", bufs=UH_RAW_BUFS))
+        uh_pool = ctx.enter_context(tc.tile_pool(name="uh", bufs=2))
+        gates = ctx.enter_context(tc.tile_pool(name="gates", bufs=BATCH_TILES))
+        z_banks = ctx.enter_context(tc.psum_pool(name="z_banks", bufs=4))
+        t_banks = ctx.enter_context(tc.psum_pool(name="t_banks", bufs=4))
+        ctx.enter_context(tc.manual_schedule())
+
+        identity = keep.tile([P, P], F32)
+        ones = keep.tile([P, P], BF16)
+        table_warmer = keep.tile([P, 1], F32)
+        bias_rows = keep.tile([P, GATES * FEATURES], BF16)
+        bias = keep.tile([P, GATES * FEATURES], F32)
+        x_raw = keep.tile([P, BATCH_TILES, FEATURES], BF16)
+        h_raw = keep.tile([P, BATCH_TILES, FEATURES], BF16)
+        c_old = keep.tile([P, BATCH_TILES, FEATURES], BF16)
+        x_codes = keep.tile([P, BATCH_TILES, PASSES, P], U32, align_bytes=64)
+        x_scales = keep.tile([P, BATCH_TILES, PASSES, P], U8, align_bytes=64)
+        h_codes = keep.tile([P, BATCH_TILES, PASSES, P], U32, align_bytes=64)
+        h_scales = keep.tile([P, BATCH_TILES, PASSES, P], U8, align_bytes=64)
+        wx_words = keep.tile([P, GATES * PASSES, 2 * FEATURES], U8, align_bytes=64)
+        wx_scales = keep.tile([P, GATES * PASSES, FEATURES], U8, align_bytes=64)
+
+        nc.vector.memset(table_warmer[:], 0.0)
+        nc.scalar.activation(out=table_warmer[:], in_=table_warmer[:], func=ACT.Sigmoid)
+        nc.vector.memset(wx_scales[:].rearrange("p j n -> p (j n)").bitcast(I32), 0)
+        nc.vector.memset(bias_rows[:].bitcast(I32), 0)
+        make_identity(nc, identity[:])
+        nc.gpsimd.memset(ones[:], 1.0)
+
+        def load_wx_words(gate):
+            passes = slice(PASSES * gate, PASSES * (gate + 1))
+            nc.sync.dma_start(
+                out=wx_words[:, passes, :].bitcast(I32),
+                in_=Wx_words[passes].rearrange("j p w -> p j w").bitcast(I32),
+            )
+
+        uh_raw = {}
+
+        def load_uh(chunk):
+            half, gate = chunk // GATES, GATE_ORDER[chunk % GATES]
+            raw = uh_raw_pool.tile([P, ROW_TILES, FEATURES], BF16)
+            nc.sync.dma_start(
+                out=raw[:],
+                in_=Uh[gate, N_TILE * half : N_TILE * (half + 1), :].rearrange("(r p) k -> p r k", p=P),
+            )
+            uh_raw[chunk] = raw
+
+        nc.scalar.dma_start(out=bias_rows[0:1, :], in_=bW.rearrange("(o g) n -> o (g n)", o=1))
+        nc.scalar.dma_start(out=bias_rows[1:2, :], in_=bU.rearrange("(o g) n -> o (g n)", o=1))
+        for b in range(BATCH_TILES):
+            nc.sync.dma_start(out=x_raw[:, b, :], in_=x_t[P * b : P * (b + 1), :])
+        for q in range(8):
+            nc.sync.dma_start(
+                out=wx_scales[32 * (q // 4) + q % 4 : P : 64].bitcast(I32),
+                in_=Wx_scales[:, q : 16 : 8, :].rearrange("j q n -> q j n").bitcast(I32),
+            )
+        load_wx_words(GATE_ORDER[0])
+        for b in range(BATCH_TILES):
+            nc.sync.dma_start(out=h_raw[:, b, :], in_=h_pre[P * b : P * (b + 1), :])
+        load_uh(0)
+        load_uh(1)
+        load_wx_words(GATE_ORDER[1])
+        load_uh(2)
+        load_wx_words(GATE_ORDER[2])
+        nc.sync.dma_start(out=c_old[:], in_=c_pre.rearrange("(b p) n -> p b n", p=P))
+        load_uh(3)
+        load_wx_words(GATE_ORDER[3])
+
+        for j in range(GATES * HALVES):
+            cols = slice(N_TILE * j, N_TILE * (j + 1))
+            spread = z_banks.tile([P, N_TILE], F32, tag="z")
+            nc.tensor.matmul(out=spread[:], lhsT=ones[:], rhs=bias_rows[:, cols], start=True, stop=True)
+            nc.scalar.copy(out=bias[:, cols], in_=spread[:])
+
+        def transpose_rows(rows, every_second_word):
+            words = rows.bitcast(F32)
+            bank = t_banks.tile([P, 2 * PASSES, P], F32, tag="bank")
+            for g in range(PASSES):
+                for u in range(2):
+                    if every_second_word:
+                        cols = words[:, (WORDS // PASSES) * g + u : (WORDS // PASSES) * (g + 1) : 2]
+                    else:
+                        cols = words[:, (WORDS // PASSES) * g + P * u : (WORDS // PASSES) * g + P * (u + 1)]
+                    nc.tensor.transpose(bank[:, 2 * g + u, :], cols, identity[:])
+            return bank
+
+        def side_by_side(bank):
+            return bank[:].rearrange("p (g u) r -> p g r u", u=2)
+
+        def quantise_activations(raw, every_second_word, copy, codes, scales):
+            grouped = {}
+            for b in range(BATCH_TILES + 1):
+                if b < BATCH_TILES:
+                    bank = transpose_rows(raw[:, b, :], every_second_word)
+                    four_k = stage.tile([P, 4 * PASSES * P], BF16, align_bytes=64)
+                    copy(
+                        out=four_k[:].bitcast(F32).rearrange("p (g r u) -> p g r u", g=PASSES, u=2),
+                        in_=side_by_side(bank),
+                    )
+                    grouped[b] = four_k
+                if b > 0:
+                    nc.vector.quantize_mx(
+                        out=codes[:, b - 1].rearrange("p g r -> p (g r)").bitcast(FP8X4),
+                        scales=scales[:, b - 1].rearrange("p g r -> p (g r)"),
+                        in_=grouped[b - 1][:],
+                    )
+
+        quantise_activations(x_raw, True, nc.vector.tensor_copy, x_codes, x_scales)
+        quantise_activations(h_raw, False, nc.scalar.copy, h_codes, h_scales)
+
+        uh_grouped = {}
+        uh_codes = {}
+        uh_scales = {}
+
+        def transpose_uh(chunk):
+            four_k = uh_pool.tile([P, 4 * PASSES * N_TILE], BF16, align_bytes=64)
+            slots = four_k[:].bitcast(F32).rearrange("p (g n u) -> p g n u", g=PASSES, u=2)
+            for r in range(ROW_TILES):
+                bank = transpose_rows(uh_raw[chunk][:, r, :], False)
+                nc.scalar.copy(out=slots[:, :, P * r : P * (r + 1), :], in_=side_by_side(bank))
+            uh_grouped[chunk] = four_k
+
+        def quantise_uh(chunk):
+            codes = uh_pool.tile([P, PASSES, N_TILE], U32, align_bytes=64)
+            scales = uh_pool.tile([P, PASSES, N_TILE], U8, align_bytes=64)
+            nc.vector.quantize_mx(
+                out=codes[:].rearrange("p g n -> p (g n)").bitcast(FP8X4),
+                scales=scales[:].rearrange("p g n -> p (g n)"),
+                in_=uh_grouped[chunk][:],
+            )
+            uh_codes[chunk] = codes
+            uh_scales[chunk] = scales
+
+        transpose_uh(0)
+        quantise_uh(0)
+
+        def place(step):
+            chunk, b = divmod(step, BATCH_TILES)
+            return chunk // GATES, GATE_ORDER[chunk % GATES], b
+
+        live = {}
+
+        def multiply(step):
+            half, gate, b = place(step)
+            chunk = step // BATCH_TILES
+            z = z_banks.tile([P, N_TILE], F32, tag="z")
+            for g in range(PASSES):
+                nc.tensor.matmul_mx(
+                    out=z[:],
+                    lhsT=x_codes[:, b, g, :].bitcast(FP8X4),
+                    lhsT_scale=x_scales[:, b, g, :],
+                    rhs=wx_words[:, PASSES * gate + g, 2 * N_TILE * half : 2 * N_TILE * (half + 1)].bitcast(FP4X4),
+                    rhs_scale=wx_scales[:, PASSES * gate + g, N_TILE * half : N_TILE * (half + 1)],
+                    start=(g == 0),
+                    stop=False,
+                )
+            for g in range(PASSES):
+                nc.tensor.matmul_mx(
+                    out=z[:],
+                    lhsT=h_codes[:, b, g, :].bitcast(FP8X4),
+                    lhsT_scale=h_scales[:, b, g, :],
+                    rhs=uh_codes[chunk][:, g, :].bitcast(FP8X4),
+                    rhs_scale=uh_scales[chunk][:, g, :],
+                    start=False,
+                    stop=(g == PASSES - 1),
+                )
+            return z
+
+        def add_bias(step, z):
+            half, gate, b = place(step)
+            first = FEATURES * gate + N_TILE * half
+            value = gates.tile([P, N_TILE], F32, tag="gate%d" % gate)
+            nc.vector.tensor_tensor(out=value[:], in0=z[:], in1=bias[:, first : first + N_TILE], op=ALU.add)
+            live[(gate, b)] = value
+
+        def squash(step):
+            half, gate, b = place(step)
+            value = live[(gate, b)]
+            nc.scalar.activation(out=value[:], in_=value[:], func=ACT.Tanh if gate == GATE_G else ACT.Sigmoid)
+
+        def multiply_gates(step):
+            half, gate, b = place(step)
+            cols = slice(N_TILE * half, N_TILE * (half + 1))
+            value = live[(gate, b)]
+            if gate == GATE_G:
+                nc.gpsimd.tensor_tensor(out=value[:], in0=value[:], in1=live[(GATE_I, b)][:], op=ALU.mult)
+            if gate == GATE_F:
+                nc.gpsimd.tensor_tensor(out=value[:], in0=value[:], in1=c_old[:, b, cols], op=ALU.mult)
+            if gate == GATE_O:
+                nc.vector.tensor_tensor(out=value[:], in0=value[:], in1=live[("tanh", b)][:], op=ALU.mult)
+                nc.sync.dma_start(out=out_0[P * b : P * (b + 1), cols], in_=value[:])
+
+        def add_cell(step):
+            half, gate, b = place(step)
+            if gate == GATE_F:
+                cell = live[(GATE_F, b)]
+                nc.vector.tensor_tensor(out=cell[:], in0=cell[:], in1=live[(GATE_G, b)][:], op=ALU.add)
+                nc.sync.dma_start(out=out_1[P * b : P * (b + 1), N_TILE * half : N_TILE * (half + 1)], in_=cell[:])
+
+        def squash_cell(step):
+            half, gate, b = place(step)
+            if gate == GATE_F:
+                squashed = gates.tile([P, N_TILE], F32, tag="tanh")
+                nc.scalar.activation(out=squashed[:], in_=live[(GATE_F, b)][:], func=ACT.Tanh)
+                live[("tanh", b)] = squashed
+
+        for step in range(STEPS + 3):
+            if step < STEPS:
+                chunk, b = divmod(step, BATCH_TILES)
+                if b == 0 and chunk + UH_RAW_BUFS < CHUNKS:
+                    load_uh(chunk + UH_RAW_BUFS)
+                if b == TRANSPOSE_AT and chunk + 1 < CHUNKS:
+                    transpose_uh(chunk + 1)
+                add_bias(step, multiply(step))
+            if 3 <= step:
+                squash_cell(step - 3)
+            if step < STEPS:
+                squash(step)
+            if 2 <= step < STEPS + 2:
+                add_cell(step - 2)
+            if 1 <= step < STEPS + 1:
+                multiply_gates(step - 1)
+            if step < STEPS and step % BATCH_TILES == QUANTISE_AT and step // BATCH_TILES + 1 < CHUNKS:
+                quantise_uh(step // BATCH_TILES + 1)

@@ -36,6 +36,9 @@ STEPS = CHUNKS * BATCH_TILES
 UH_RAW_BUFS = 4
 TRANSPOSE_AT = 1
 QUANTISE_AT = 3
+PRODUCT_LAG = 1
+CELL_LAG = 2
+TANH_LAG = 5
 
 FLOPS = 2 * BATCH * (2 * FEATURES) * (GATES * FEATURES)
 
@@ -67,10 +70,12 @@ def tile_lstmcell_e_kernel(tc, x_t, h_pre, c_pre, Wx_words, Wx_scales, bW, Uh, b
         wx_words = keep.tile([P, GATES * PASSES, 2 * FEATURES], U8, align_bytes=64)
         wx_scales = keep.tile([P, GATES * PASSES, FEATURES], U8, align_bytes=64)
 
+        nc.vector.memset(bias_rows[:].bitcast(I32), 0)
+        nc.scalar.dma_start(out=bias_rows[0:1, :], in_=bW.rearrange("(o g) n -> o (g n)", o=1))
+        nc.scalar.dma_start(out=bias_rows[1:2, :], in_=bU.rearrange("(o g) n -> o (g n)", o=1))
         nc.vector.memset(table_warmer[:], 0.0)
         nc.scalar.activation(out=table_warmer[:], in_=table_warmer[:], func=ACT.Sigmoid)
         nc.vector.memset(wx_scales[:].rearrange("p j n -> p (j n)").bitcast(I32), 0)
-        nc.vector.memset(bias_rows[:].bitcast(I32), 0)
         make_identity(nc, identity[:])
         nc.gpsimd.memset(ones[:], 1.0)
 
@@ -92,10 +97,9 @@ def tile_lstmcell_e_kernel(tc, x_t, h_pre, c_pre, Wx_words, Wx_scales, bW, Uh, b
             )
             uh_raw[chunk] = raw
 
-        nc.scalar.dma_start(out=bias_rows[0:1, :], in_=bW.rearrange("(o g) n -> o (g n)", o=1))
-        nc.scalar.dma_start(out=bias_rows[1:2, :], in_=bU.rearrange("(o g) n -> o (g n)", o=1))
         for b in range(BATCH_TILES):
             nc.sync.dma_start(out=x_raw[:, b, :], in_=x_t[P * b : P * (b + 1), :])
+        load_uh(0)
         for q in range(8):
             nc.sync.dma_start(
                 out=wx_scales[32 * (q // 4) + q % 4 : P : 64].bitcast(I32),
@@ -104,7 +108,6 @@ def tile_lstmcell_e_kernel(tc, x_t, h_pre, c_pre, Wx_words, Wx_scales, bW, Uh, b
         load_wx_words(GATE_ORDER[0])
         for b in range(BATCH_TILES):
             nc.sync.dma_start(out=h_raw[:, b, :], in_=h_pre[P * b : P * (b + 1), :])
-        load_uh(0)
         load_uh(1)
         load_wx_words(GATE_ORDER[1])
         load_uh(2)
@@ -112,12 +115,6 @@ def tile_lstmcell_e_kernel(tc, x_t, h_pre, c_pre, Wx_words, Wx_scales, bW, Uh, b
         nc.sync.dma_start(out=c_old[:], in_=c_pre.rearrange("(b p) n -> p b n", p=P))
         load_uh(3)
         load_wx_words(GATE_ORDER[3])
-
-        for j in range(GATES * HALVES):
-            cols = slice(N_TILE * j, N_TILE * (j + 1))
-            spread = z_banks.tile([P, N_TILE], F32, tag="z")
-            nc.tensor.matmul(out=spread[:], lhsT=ones[:], rhs=bias_rows[:, cols], start=True, stop=True)
-            nc.scalar.copy(out=bias[:, cols], in_=spread[:])
 
         def transpose_rows(rows, every_second_word):
             words = rows.bitcast(F32)
@@ -153,7 +150,15 @@ def tile_lstmcell_e_kernel(tc, x_t, h_pre, c_pre, Wx_words, Wx_scales, bW, Uh, b
                     )
 
         quantise_activations(x_raw, True, nc.vector.tensor_copy, x_codes, x_scales)
-        quantise_activations(h_raw, False, nc.scalar.copy, h_codes, h_scales)
+
+        for j in range(GATES * HALVES):
+            cols = slice(N_TILE * j, N_TILE * (j + 1))
+            spread = z_banks.tile([P, N_TILE], F32, tag="z")
+            nc.tensor.matmul(out=spread[:], lhsT=ones[:], rhs=bias_rows[:, cols], start=True, stop=True)
+            if j % 2 == 0:
+                nc.scalar.copy(out=bias[:, cols], in_=spread[:])
+            else:
+                nc.vector.tensor_copy(out=bias[:, cols], in_=spread[:])
 
         uh_grouped = {}
         uh_codes = {}
@@ -180,6 +185,7 @@ def tile_lstmcell_e_kernel(tc, x_t, h_pre, c_pre, Wx_words, Wx_scales, bW, Uh, b
 
         transpose_uh(0)
         quantise_uh(0)
+        quantise_activations(h_raw, False, nc.scalar.copy, h_codes, h_scales)
 
         def place(step):
             chunk, b = divmod(step, BATCH_TILES)
@@ -232,7 +238,7 @@ def tile_lstmcell_e_kernel(tc, x_t, h_pre, c_pre, Wx_words, Wx_scales, bW, Uh, b
             if gate == GATE_G:
                 nc.gpsimd.tensor_tensor(out=value[:], in0=value[:], in1=live[(GATE_I, b)][:], op=ALU.mult)
             if gate == GATE_F:
-                nc.gpsimd.tensor_tensor(out=value[:], in0=value[:], in1=c_old[:, b, cols], op=ALU.mult)
+                nc.vector.tensor_tensor(out=value[:], in0=value[:], in1=c_old[:, b, cols], op=ALU.mult)
             if gate == GATE_O:
                 nc.vector.tensor_tensor(out=value[:], in0=value[:], in1=live[("tanh", b)][:], op=ALU.mult)
                 nc.sync.dma_start(out=out_0[P * b : P * (b + 1), cols], in_=value[:])
@@ -241,7 +247,7 @@ def tile_lstmcell_e_kernel(tc, x_t, h_pre, c_pre, Wx_words, Wx_scales, bW, Uh, b
             half, gate, b = place(step)
             if gate == GATE_F:
                 cell = live[(GATE_F, b)]
-                nc.vector.tensor_tensor(out=cell[:], in0=cell[:], in1=live[(GATE_G, b)][:], op=ALU.add)
+                nc.gpsimd.tensor_tensor(out=cell[:], in0=cell[:], in1=live[(GATE_G, b)][:], op=ALU.add)
                 nc.sync.dma_start(out=out_1[P * b : P * (b + 1), N_TILE * half : N_TILE * (half + 1)], in_=cell[:])
 
         def squash_cell(step):
@@ -251,7 +257,7 @@ def tile_lstmcell_e_kernel(tc, x_t, h_pre, c_pre, Wx_words, Wx_scales, bW, Uh, b
                 nc.scalar.activation(out=squashed[:], in_=live[(GATE_F, b)][:], func=ACT.Tanh)
                 live[("tanh", b)] = squashed
 
-        for step in range(STEPS + 3):
+        for step in range(STEPS + TANH_LAG):
             if step < STEPS:
                 chunk, b = divmod(step, BATCH_TILES)
                 if b == 0 and chunk + UH_RAW_BUFS < CHUNKS:
@@ -259,13 +265,13 @@ def tile_lstmcell_e_kernel(tc, x_t, h_pre, c_pre, Wx_words, Wx_scales, bW, Uh, b
                 if b == TRANSPOSE_AT and chunk + 1 < CHUNKS:
                     transpose_uh(chunk + 1)
                 add_bias(step, multiply(step))
-            if 3 <= step:
-                squash_cell(step - 3)
+            if 0 <= step - TANH_LAG < STEPS:
+                squash_cell(step - TANH_LAG)
             if step < STEPS:
                 squash(step)
-            if 2 <= step < STEPS + 2:
-                add_cell(step - 2)
-            if 1 <= step < STEPS + 1:
-                multiply_gates(step - 1)
+            if 0 <= step - CELL_LAG < STEPS:
+                add_cell(step - CELL_LAG)
+            if 0 <= step - PRODUCT_LAG < STEPS:
+                multiply_gates(step - PRODUCT_LAG)
             if step < STEPS and step % BATCH_TILES == QUANTISE_AT and step // BATCH_TILES + 1 < CHUNKS:
                 quantise_uh(step // BATCH_TILES + 1)

@@ -34,10 +34,8 @@ CHUNKS = HALVES * GATES
 STEPS = CHUNKS * BATCH_TILES
 
 UH_RAW_BUFS = 4
-TRANSPOSE_AT = 1
-QUANTISE_AT = 3
-PRODUCT_LAG = 1
-CELL_LAG = 2
+PRODUCT_LAG = 2
+CELL_LAG = 3
 TANH_LAG = 5
 
 FLOPS = 2 * BATCH * (2 * FEATURES) * (GATES * FEATURES)
@@ -257,14 +255,19 @@ def tile_lstmcell_e_kernel(tc, x_t, h_pre, c_pre, Wx_words, Wx_scales, bW, Uh, b
                 nc.scalar.activation(out=squashed[:], in_=live[(GATE_F, b)][:], func=ACT.Tanh)
                 live[("tanh", b)] = squashed
 
+        transposed_before = {}
+        for chunk in range(1, CHUNKS):
+            transposed_before[max(1, BATCH_TILES * (chunk - 1))] = chunk
         for step in range(STEPS + TANH_LAG):
             if step < STEPS:
                 chunk, b = divmod(step, BATCH_TILES)
                 if b == 0 and chunk + UH_RAW_BUFS < CHUNKS:
                     load_uh(chunk + UH_RAW_BUFS)
-                if b == TRANSPOSE_AT and chunk + 1 < CHUNKS:
-                    transpose_uh(chunk + 1)
+                if step in transposed_before:
+                    transpose_uh(transposed_before[step])
                 add_bias(step, multiply(step))
+                if step - 1 in transposed_before:
+                    quantise_uh(transposed_before[step - 1])
             if 0 <= step - TANH_LAG < STEPS:
                 squash_cell(step - TANH_LAG)
             if step < STEPS:
@@ -273,5 +276,3 @@ def tile_lstmcell_e_kernel(tc, x_t, h_pre, c_pre, Wx_words, Wx_scales, bW, Uh, b
                 add_cell(step - CELL_LAG)
             if 0 <= step - PRODUCT_LAG < STEPS:
                 multiply_gates(step - PRODUCT_LAG)
-            if step < STEPS and step % BATCH_TILES == QUANTISE_AT and step // BATCH_TILES + 1 < CHUNKS:
-                quantise_uh(step // BATCH_TILES + 1)

@@ -27,12 +27,14 @@ N_TILE = 512
 HALVES = FEATURES // N_TILE
 BATCH_TILES = BATCH // P
 ROW_TILES = N_TILE // P
-WORDS = FEATURES // 2
+PASS_WORDS = K_PASS // 2
 
 GATE_ORDER = (GATE_I, GATE_G, GATE_F, GATE_O)
 CHUNKS = HALVES * GATES
 STEPS = CHUNKS * BATCH_TILES
 
+Z_BANKS = 4
+RUN = 2
 UH_RAW_BUFS = 4
 PRODUCT_LAG = 2
 CELL_LAG = 3
@@ -49,7 +51,7 @@ def tile_lstmcell_e_kernel(tc, x_t, h_pre, c_pre, Wx_words, Wx_scales, bW, Uh, b
         uh_raw_pool = ctx.enter_context(tc.tile_pool(name="uh_raw", bufs=UH_RAW_BUFS))
         uh_pool = ctx.enter_context(tc.tile_pool(name="uh", bufs=2))
         gates = ctx.enter_context(tc.tile_pool(name="gates", bufs=BATCH_TILES))
-        z_banks = ctx.enter_context(tc.psum_pool(name="z_banks", bufs=4))
+        z_banks = ctx.enter_context(tc.psum_pool(name="z_banks", bufs=Z_BANKS))
         t_banks = ctx.enter_context(tc.psum_pool(name="t_banks", bufs=4))
         ctx.enter_context(tc.manual_schedule())
 
@@ -120,9 +122,9 @@ def tile_lstmcell_e_kernel(tc, x_t, h_pre, c_pre, Wx_words, Wx_scales, bW, Uh, b
             for g in range(PASSES):
                 for u in range(2):
                     if every_second_word:
-                        cols = words[:, (WORDS // PASSES) * g + u : (WORDS // PASSES) * (g + 1) : 2]
+                        cols = words[:, PASS_WORDS * g + u : PASS_WORDS * (g + 1) : 2]
                     else:
-                        cols = words[:, (WORDS // PASSES) * g + P * u : (WORDS // PASSES) * g + P * (u + 1)]
+                        cols = words[:, PASS_WORDS * g + P * u : PASS_WORDS * g + P * (u + 1)]
                     nc.tensor.transpose(bank[:, 2 * g + u, :], cols, identity[:])
             return bank
 
@@ -147,17 +149,6 @@ def tile_lstmcell_e_kernel(tc, x_t, h_pre, c_pre, Wx_words, Wx_scales, bW, Uh, b
                         in_=grouped[b - 1][:],
                     )
 
-        quantise_activations(x_raw, True, nc.vector.tensor_copy, x_codes, x_scales)
-
-        for j in range(GATES * HALVES):
-            cols = slice(N_TILE * j, N_TILE * (j + 1))
-            spread = z_banks.tile([P, N_TILE], F32, tag="z")
-            nc.tensor.matmul(out=spread[:], lhsT=ones[:], rhs=bias_rows[:, cols], start=True, stop=True)
-            if j % 2 == 0:
-                nc.scalar.copy(out=bias[:, cols], in_=spread[:])
-            else:
-                nc.vector.tensor_copy(out=bias[:, cols], in_=spread[:])
-
         uh_grouped = {}
         uh_codes = {}
         uh_scales = {}
@@ -181,6 +172,17 @@ def tile_lstmcell_e_kernel(tc, x_t, h_pre, c_pre, Wx_words, Wx_scales, bW, Uh, b
             uh_codes[chunk] = codes
             uh_scales[chunk] = scales
 
+        quantise_activations(x_raw, True, nc.vector.tensor_copy, x_codes, x_scales)
+
+        for j in range(GATES * HALVES):
+            cols = slice(N_TILE * j, N_TILE * (j + 1))
+            spread = z_banks.tile([P, N_TILE], F32, tag="z")
+            nc.tensor.matmul(out=spread[:], lhsT=ones[:], rhs=bias_rows[:, cols], start=True, stop=True)
+            if j % 2 == 0:
+                nc.scalar.copy(out=bias[:, cols], in_=spread[:])
+            else:
+                nc.vector.tensor_copy(out=bias[:, cols], in_=spread[:])
+
         transpose_uh(0)
         quantise_uh(0)
         quantise_activations(h_raw, False, nc.scalar.copy, h_codes, h_scales)
@@ -189,11 +191,11 @@ def tile_lstmcell_e_kernel(tc, x_t, h_pre, c_pre, Wx_words, Wx_scales, bW, Uh, b
             chunk, b = divmod(step, BATCH_TILES)
             return chunk // GATES, GATE_ORDER[chunk % GATES], b
 
+        sums = {}
         live = {}
 
-        def multiply(step):
+        def multiply_x(step):
             half, gate, b = place(step)
-            chunk = step // BATCH_TILES
             z = z_banks.tile([P, N_TILE], F32, tag="z")
             for g in range(PASSES):
                 nc.tensor.matmul_mx(
@@ -205,9 +207,13 @@ def tile_lstmcell_e_kernel(tc, x_t, h_pre, c_pre, Wx_words, Wx_scales, bW, Uh, b
                     start=(g == 0),
                     stop=False,
                 )
+            sums[step] = z
+
+        def multiply_h(step):
+            chunk, b = divmod(step, BATCH_TILES)
             for g in range(PASSES):
                 nc.tensor.matmul_mx(
-                    out=z[:],
+                    out=sums[step][:],
                     lhsT=h_codes[:, b, g, :].bitcast(FP8X4),
                     lhsT_scale=h_scales[:, b, g, :],
                     rhs=uh_codes[chunk][:, g, :].bitcast(FP8X4),
@@ -215,13 +221,12 @@ def tile_lstmcell_e_kernel(tc, x_t, h_pre, c_pre, Wx_words, Wx_scales, bW, Uh, b
                     start=False,
                     stop=(g == PASSES - 1),
                 )
-            return z
 
-        def add_bias(step, z):
+        def add_bias(step):
             half, gate, b = place(step)
             first = FEATURES * gate + N_TILE * half
             value = gates.tile([P, N_TILE], F32, tag="gate%d" % gate)
-            nc.vector.tensor_tensor(out=value[:], in0=z[:], in1=bias[:, first : first + N_TILE], op=ALU.add)
+            nc.vector.tensor_tensor(out=value[:], in0=sums[step][:], in1=bias[:, first : first + N_TILE], op=ALU.add)
             live[(gate, b)] = value
 
         def squash(step):
@@ -257,15 +262,21 @@ def tile_lstmcell_e_kernel(tc, x_t, h_pre, c_pre, Wx_words, Wx_scales, bW, Uh, b
 
         transposed_before = {}
         for chunk in range(1, CHUNKS):
-            transposed_before[max(1, BATCH_TILES * (chunk - 1))] = chunk
+            ahead = BATCH_TILES * (chunk - 1)
+            transposed_before[max(RUN, ahead - ahead % RUN)] = chunk
+
         for step in range(STEPS + TANH_LAG):
             if step < STEPS:
                 chunk, b = divmod(step, BATCH_TILES)
                 if b == 0 and chunk + UH_RAW_BUFS < CHUNKS:
                     load_uh(chunk + UH_RAW_BUFS)
-                if step in transposed_before:
-                    transpose_uh(transposed_before[step])
-                add_bias(step, multiply(step))
+                if step % RUN == 0:
+                    if step in transposed_before:
+                        transpose_uh(transposed_before[step])
+                    for member in range(step, min(step + RUN, STEPS)):
+                        multiply_x(member)
+                multiply_h(step)
+                add_bias(step)
                 if step - 1 in transposed_before:
                     quantise_uh(transposed_before[step - 1])
             if 0 <= step - TANH_LAG < STEPS:

@@ -239,7 +239,7 @@ def tile_lstmcell_e_kernel(tc, x_t, h_pre, c_pre, Wx_words, Wx_scales, bW, Uh, b
             cols = slice(N_TILE * half, N_TILE * (half + 1))
             value = live[(gate, b)]
             if gate == GATE_G:
-                nc.gpsimd.tensor_tensor(out=value[:], in0=value[:], in1=live[(GATE_I, b)][:], op=ALU.mult)
+                nc.vector.tensor_tensor(out=value[:], in0=value[:], in1=live[(GATE_I, b)][:], op=ALU.mult)
             if gate == GATE_F:
                 nc.vector.tensor_tensor(out=value[:], in0=value[:], in1=c_old[:, b, cols], op=ALU.mult)
             if gate == GATE_O:
@@ -250,7 +250,7 @@ def tile_lstmcell_e_kernel(tc, x_t, h_pre, c_pre, Wx_words, Wx_scales, bW, Uh, b
             half, gate, b = place(step)
             if gate == GATE_F:
                 cell = live[(GATE_F, b)]
-                nc.gpsimd.tensor_tensor(out=cell[:], in0=cell[:], in1=live[(GATE_G, b)][:], op=ALU.add)
+                nc.vector.tensor_tensor(out=cell[:], in0=cell[:], in1=live[(GATE_G, b)][:], op=ALU.add)
                 nc.sync.dma_start(out=out_1[P * b : P * (b + 1), N_TILE * half : N_TILE * (half + 1)], in_=cell[:])
 
         def squash_cell(step):

@@ -39,6 +39,7 @@ UH_RAW_BUFS = 4
 PRODUCT_LAG = 2
 CELL_LAG = 3
 TANH_LAG = 5
+SPREAD = 5
 
 FLOPS = 2 * BATCH * (2 * FEATURES) * (GATES * FEATURES)
 
@@ -239,7 +240,7 @@ def tile_lstmcell_e_kernel(tc, x_t, h_pre, c_pre, Wx_words, Wx_scales, bW, Uh, b
             cols = slice(N_TILE * half, N_TILE * (half + 1))
             value = live[(gate, b)]
             if gate == GATE_G:
-                nc.vector.tensor_tensor(out=value[:], in0=value[:], in1=live[(GATE_I, b)][:], op=ALU.mult)
+                nc.gpsimd.tensor_tensor(out=value[:], in0=value[:], in1=live[(GATE_I, b)][:], op=ALU.mult)
             if gate == GATE_F:
                 nc.vector.tensor_tensor(out=value[:], in0=value[:], in1=c_old[:, b, cols], op=ALU.mult)
             if gate == GATE_O:
@@ -265,6 +266,19 @@ def tile_lstmcell_e_kernel(tc, x_t, h_pre, c_pre, Wx_words, Wx_scales, bW, Uh, b
             ahead = BATCH_TILES * (chunk - 1)
             transposed_before[max(RUN, ahead - ahead % RUN)] = chunk
 
+        def due(kind, step):
+            found = []
+            for s in range(max(0, step - 16), min(step + 1, STEPS)):
+                half, gate, b = place(s)
+                late = SPREAD if half < HALVES - 1 else 0
+                if kind == "cell" and gate == GATE_F and s + CELL_LAG + late - 1 * (late > 0) == step:
+                    found.append(s)
+                if kind == "tanh" and gate == GATE_F and s + TANH_LAG + late - 2 * (late > 0) == step:
+                    found.append(s)
+                if kind == "product" and s + PRODUCT_LAG + (late if gate == GATE_O else 0) == step:
+                    found.append(s)
+            return found
+
         for step in range(STEPS + TANH_LAG):
             if step < STEPS:
                 chunk, b = divmod(step, BATCH_TILES)
@@ -279,11 +293,11 @@ def tile_lstmcell_e_kernel(tc, x_t, h_pre, c_pre, Wx_words, Wx_scales, bW, Uh, b
                 add_bias(step)
                 if step - 1 in transposed_before:
                     quantise_uh(transposed_before[step - 1])
-            if 0 <= step - TANH_LAG < STEPS:
-                squash_cell(step - TANH_LAG)
+            for s in due("tanh", step):
+                squash_cell(s)
             if step < STEPS:
                 squash(step)
-            if 0 <= step - CELL_LAG < STEPS:
-                add_cell(step - CELL_LAG)
-            if 0 <= step - PRODUCT_LAG < STEPS:
-                multiply_gates(step - PRODUCT_LAG)
+            for s in due("cell", step):
+                add_cell(s)
+            for s in due("product", step):
+                multiply_gates(s)

@@ -29,17 +29,21 @@ BATCH_TILES = BATCH // P
 ROW_TILES = N_TILE // P
 PASS_WORDS = K_PASS // 2
 
-GATE_ORDER = (GATE_I, GATE_G, GATE_F, GATE_O)
 CHUNKS = HALVES * GATES
 STEPS = CHUNKS * BATCH_TILES
 
-Z_BANKS = 4
 RUN = 2
 UH_RAW_BUFS = 4
+UH_CODE_BUFS = 6
 PRODUCT_LAG = 2
-CELL_LAG = 3
-TANH_LAG = 5
-SPREAD = 5
+CELL_LAG = 1
+TANH_LAG = 2
+DRAIN = 8
+
+HALF_GATES = ((GATE_I, GATE_G, GATE_F, GATE_O), (GATE_I, GATE_G, GATE_F, GATE_O))
+HALF_GROUPS = (((0, 1, 2, 3, 4),), ((0,), (1,), (2,), (3,), (4,)))
+LEAD = 5
+QUANT_LAG = 1
 
 FLOPS = 2 * BATCH * (2 * FEATURES) * (GATES * FEATURES)
 
@@ -51,8 +55,9 @@ def tile_lstmcell_e_kernel(tc, x_t, h_pre, c_pre, Wx_words, Wx_scales, bW, Uh, b
         stage = ctx.enter_context(tc.tile_pool(name="stage", bufs=3))
         uh_raw_pool = ctx.enter_context(tc.tile_pool(name="uh_raw", bufs=UH_RAW_BUFS))
         uh_pool = ctx.enter_context(tc.tile_pool(name="uh", bufs=2))
+        uh_code_pool = ctx.enter_context(tc.tile_pool(name="uh_code", bufs=UH_CODE_BUFS))
         gates = ctx.enter_context(tc.tile_pool(name="gates", bufs=BATCH_TILES))
-        z_banks = ctx.enter_context(tc.psum_pool(name="z_banks", bufs=Z_BANKS))
+        z_banks = ctx.enter_context(tc.psum_pool(name="z_banks", bufs=4))
         t_banks = ctx.enter_context(tc.psum_pool(name="t_banks", bufs=4))
         ctx.enter_context(tc.manual_schedule())
 
@@ -80,6 +85,12 @@ def tile_lstmcell_e_kernel(tc, x_t, h_pre, c_pre, Wx_words, Wx_scales, bW, Uh, b
         make_identity(nc, identity[:])
         nc.gpsimd.memset(ones[:], 1.0)
 
+        def chunk_of(half, gate):
+            return GATES * half + HALF_GATES[half].index(gate)
+
+        def gate_of(chunk):
+            return HALF_GATES[chunk // GATES][chunk % GATES]
+
         def load_wx_words(gate):
             passes = slice(PASSES * gate, PASSES * (gate + 1))
             nc.sync.dma_start(
@@ -90,7 +101,7 @@ def tile_lstmcell_e_kernel(tc, x_t, h_pre, c_pre, Wx_words, Wx_scales, bW, Uh, b
         uh_raw = {}
 
         def load_uh(chunk):
-            half, gate = chunk // GATES, GATE_ORDER[chunk % GATES]
+            half, gate = chunk // GATES, gate_of(chunk)
             raw = uh_raw_pool.tile([P, ROW_TILES, FEATURES], BF16)
             nc.sync.dma_start(
                 out=raw[:],
@@ -106,16 +117,14 @@ def tile_lstmcell_e_kernel(tc, x_t, h_pre, c_pre, Wx_words, Wx_scales, bW, Uh, b
                 out=wx_scales[32 * (q // 4) + q % 4 : P : 64].bitcast(I32),
                 in_=Wx_scales[:, q : 16 : 8, :].rearrange("j q n -> q j n").bitcast(I32),
             )
-        load_wx_words(GATE_ORDER[0])
+        load_wx_words(gate_of(0))
         for b in range(BATCH_TILES):
             nc.sync.dma_start(out=h_raw[:, b, :], in_=h_pre[P * b : P * (b + 1), :])
-        load_uh(1)
-        load_wx_words(GATE_ORDER[1])
-        load_uh(2)
-        load_wx_words(GATE_ORDER[2])
-        nc.sync.dma_start(out=c_old[:], in_=c_pre.rearrange("(b p) n -> p b n", p=P))
-        load_uh(3)
-        load_wx_words(GATE_ORDER[3])
+        for chunk in range(1, GATES):
+            if gate_of(chunk - 1) == GATE_F:
+                nc.sync.dma_start(out=c_old[:], in_=c_pre.rearrange("(b p) n -> p b n", p=P))
+            load_uh(chunk)
+            load_wx_words(gate_of(chunk))
 
         def transpose_rows(rows, every_second_word):
             words = rows.bitcast(F32)
@@ -163,8 +172,8 @@ def tile_lstmcell_e_kernel(tc, x_t, h_pre, c_pre, Wx_words, Wx_scales, bW, Uh, b
             uh_grouped[chunk] = four_k
 
         def quantise_uh(chunk):
-            codes = uh_pool.tile([P, PASSES, N_TILE], U32, align_bytes=64)
-            scales = uh_pool.tile([P, PASSES, N_TILE], U8, align_bytes=64)
+            codes = uh_code_pool.tile([P, PASSES, N_TILE], U32, align_bytes=64)
+            scales = uh_code_pool.tile([P, PASSES, N_TILE], U8, align_bytes=64)
             nc.vector.quantize_mx(
                 out=codes[:].rearrange("p g n -> p (g n)").bitcast(FP8X4),
                 scales=scales[:].rearrange("p g n -> p (g n)"),
@@ -188,16 +197,60 @@ def tile_lstmcell_e_kernel(tc, x_t, h_pre, c_pre, Wx_words, Wx_scales, bW, Uh, b
         quantise_uh(0)
         quantise_activations(h_raw, False, nc.scalar.copy, h_codes, h_scales)
 
-        def place(step):
-            chunk, b = divmod(step, BATCH_TILES)
-            return chunk // GATES, GATE_ORDER[chunk % GATES], b
+        order = []
+        for half in range(HALVES):
+            for group in HALF_GROUPS[half]:
+                order.extend((half, gate, b) for gate in HALF_GATES[half] for b in group)
+        slot_of = dict((place, slot) for slot, place in enumerate(order))
+        first_use = {}
+        for slot, (half, gate, b) in enumerate(order):
+            first_use.setdefault(chunk_of(half, gate), slot)
+        transposed_before = {}
+        for chunk in range(CHUNKS - 1, 0, -1):
+            slot = max(RUN, first_use[chunk] - LEAD)
+            slot -= slot % RUN
+            while slot in transposed_before:
+                slot -= RUN
+            transposed_before[slot] = chunk
+        last_transposes = max(transposed_before)
+
+        due = {}
+
+        def at(slot, what, place):
+            due.setdefault(slot, []).append((what, place))
+
+        for half in range(HALVES):
+            for b in range(BATCH_TILES):
+                s_i, s_g, s_f, s_o = (slot_of[(half, gate, b)] for gate in (GATE_I, GATE_G, GATE_F, GATE_O))
+                tile_by_tile = len(HALF_GROUPS[half]) > 1
+                on_pool = tile_by_tile and b != HALF_GROUPS[half][-1][-1]
+                if tile_by_tile:
+                    t_ig = max(s_i, s_g)
+                    t_fc = s_f + 1
+                    t_cell = t_fc
+                    t_tanh = t_cell + (2 if on_pool else 1)
+                    t_out = t_cell + (6 if on_pool else 2)
+                else:
+                    t_ig = max(s_i, s_g) + PRODUCT_LAG
+                    t_fc = s_f + PRODUCT_LAG
+                    t_cell = max(t_ig, t_fc) + CELL_LAG
+                    t_tanh = t_cell + TANH_LAG
+                    t_out = max(t_tanh + 1, s_o + PRODUCT_LAG)
+                at(t_ig, "ig", (half, b))
+                at(t_fc, "fc", (half, b))
+                at(t_cell, "cell", (half, b))
+                at(t_tanh, "tanh", (half, b))
+                at(t_out, "out", (half, b))
 
         sums = {}
         live = {}
 
-        def multiply_x(step):
-            half, gate, b = place(step)
-            z = z_banks.tile([P, N_TILE], F32, tag="z")
+        def multiply_x(slot):
+            half, gate, b = order[slot]
+            if slot > last_transposes + 4 and slot % 2 == 1:
+                z = t_banks.tile([P, N_TILE], F32, tag="bank")
+            else:
+                z = z_banks.tile([P, N_TILE], F32, tag="z")
             for g in range(PASSES):
                 nc.tensor.matmul_mx(
                     out=z[:],
@@ -208,13 +261,14 @@ def tile_lstmcell_e_kernel(tc, x_t, h_pre, c_pre, Wx_words, Wx_scales, bW, Uh, b
                     start=(g == 0),
                     stop=False,
                 )
-            sums[step] = z
+            sums[slot] = z
 
-        def multiply_h(step):
-            chunk, b = divmod(step, BATCH_TILES)
+        def multiply_h(slot):
+            half, gate, b = order[slot]
+            chunk = chunk_of(half, gate)
             for g in range(PASSES):
                 nc.tensor.matmul_mx(
-                    out=sums[step][:],
+                    out=sums[slot][:],
                     lhsT=h_codes[:, b, g, :].bitcast(FP8X4),
                     lhsT_scale=h_scales[:, b, g, :],
                     rhs=uh_codes[chunk][:, g, :].bitcast(FP8X4),
@@ -223,81 +277,58 @@ def tile_lstmcell_e_kernel(tc, x_t, h_pre, c_pre, Wx_words, Wx_scales, bW, Uh, b
                     stop=(g == PASSES - 1),
                 )
 
-        def add_bias(step):
-            half, gate, b = place(step)
+        def add_bias(slot):
+            half, gate, b = order[slot]
             first = FEATURES * gate + N_TILE * half
             value = gates.tile([P, N_TILE], F32, tag="gate%d" % gate)
-            nc.vector.tensor_tensor(out=value[:], in0=sums[step][:], in1=bias[:, first : first + N_TILE], op=ALU.add)
-            live[(gate, b)] = value
+            nc.vector.tensor_tensor(out=value[:], in0=sums[slot][:], in1=bias[:, first : first + N_TILE], op=ALU.add)
+            live[(gate, half, b)] = value
 
-        def squash(step):
-            half, gate, b = place(step)
-            value = live[(gate, b)]
+        def squash(slot):
+            half, gate, b = order[slot]
+            value = live[(gate, half, b)]
             nc.scalar.activation(out=value[:], in_=value[:], func=ACT.Tanh if gate == GATE_G else ACT.Sigmoid)
 
-        def multiply_gates(step):
-            half, gate, b = place(step)
+        def epilogue(what, half, b):
             cols = slice(N_TILE * half, N_TILE * (half + 1))
-            value = live[(gate, b)]
-            if gate == GATE_G:
-                nc.gpsimd.tensor_tensor(out=value[:], in0=value[:], in1=live[(GATE_I, b)][:], op=ALU.mult)
-            if gate == GATE_F:
-                nc.vector.tensor_tensor(out=value[:], in0=value[:], in1=c_old[:, b, cols], op=ALU.mult)
-            if gate == GATE_O:
-                nc.vector.tensor_tensor(out=value[:], in0=value[:], in1=live[("tanh", b)][:], op=ALU.mult)
-                nc.sync.dma_start(out=out_0[P * b : P * (b + 1), cols], in_=value[:])
-
-        def add_cell(step):
-            half, gate, b = place(step)
-            if gate == GATE_F:
-                cell = live[(GATE_F, b)]
-                nc.vector.tensor_tensor(out=cell[:], in0=cell[:], in1=live[(GATE_G, b)][:], op=ALU.add)
-                nc.sync.dma_start(out=out_1[P * b : P * (b + 1), N_TILE * half : N_TILE * (half + 1)], in_=cell[:])
-
-        def squash_cell(step):
-            half, gate, b = place(step)
-            if gate == GATE_F:
+            rows = slice(P * b, P * (b + 1))
+            if what == "ig":
+                nc.gpsimd.tensor_tensor(out=live[(GATE_G, half, b)][:], in0=live[(GATE_G, half, b)][:], in1=live[(GATE_I, half, b)][:], op=ALU.mult)
+            if what == "fc":
+                nc.vector.tensor_tensor(out=live[(GATE_F, half, b)][:], in0=live[(GATE_F, half, b)][:], in1=c_old[:, b, cols], op=ALU.mult)
+            if what == "cell":
+                (nc.gpsimd if (half == HALVES - 1 and b != HALF_GROUPS[half][-1][-1]) else nc.vector).tensor_tensor(out=live[(GATE_F, half, b)][:], in0=live[(GATE_F, half, b)][:], in1=live[(GATE_G, half, b)][:], op=ALU.add)
+                nc.sync.dma_start(out=out_1[rows, cols], in_=live[(GATE_F, half, b)][:])
+            if what == "tanh":
                 squashed = gates.tile([P, N_TILE], F32, tag="tanh")
-                nc.scalar.activation(out=squashed[:], in_=live[(GATE_F, b)][:], func=ACT.Tanh)
-                live[("tanh", b)] = squashed
+                nc.scalar.activation(out=squashed[:], in_=live[(GATE_F, half, b)][:], func=ACT.Tanh)
+                live[("tanh", half, b)] = squashed
+            if what == "out":
+                nc.vector.tensor_tensor(out=live[(GATE_O, half, b)][:], in0=live[(GATE_O, half, b)][:], in1=live[("tanh", half, b)][:], op=ALU.mult)
+                nc.sync.dma_start(out=out_0[rows, cols], in_=live[(GATE_O, half, b)][:])
 
-        transposed_before = {}
-        for chunk in range(1, CHUNKS):
-            ahead = BATCH_TILES * (chunk - 1)
-            transposed_before[max(RUN, ahead - ahead % RUN)] = chunk
+        loaded = [UH_RAW_BUFS]
 
-        def due(kind, step):
-            found = []
-            for s in range(max(0, step - 16), min(step + 1, STEPS)):
-                half, gate, b = place(s)
-                late = SPREAD if half < HALVES - 1 else 0
-                if kind == "cell" and gate == GATE_F and s + CELL_LAG + late - 1 * (late > 0) == step:
-                    found.append(s)
-                if kind == "tanh" and gate == GATE_F and s + TANH_LAG + late - 2 * (late > 0) == step:
-                    found.append(s)
-                if kind == "product" and s + PRODUCT_LAG + (late if gate == GATE_O else 0) == step:
-                    found.append(s)
-            return found
-
-        for step in range(STEPS + TANH_LAG):
-            if step < STEPS:
-                chunk, b = divmod(step, BATCH_TILES)
-                if b == 0 and chunk + UH_RAW_BUFS < CHUNKS:
-                    load_uh(chunk + UH_RAW_BUFS)
-                if step % RUN == 0:
-                    if step in transposed_before:
-                        transpose_uh(transposed_before[step])
-                    for member in range(step, min(step + RUN, STEPS)):
+        for slot in range(STEPS + DRAIN):
+            if slot < STEPS:
+                if slot % RUN == 0:
+                    if slot in transposed_before:
+                        transpose_uh(transposed_before[slot])
+                        if loaded[0] < CHUNKS:
+                            load_uh(loaded[0])
+                            loaded[0] += 1
+                    for member in range(slot, min(slot + RUN, STEPS)):
                         multiply_x(member)
-                multiply_h(step)
-                add_bias(step)
-                if step - 1 in transposed_before:
-                    quantise_uh(transposed_before[step - 1])
-            for s in due("tanh", step):
-                squash_cell(s)
-            if step < STEPS:
-                squash(step)
-            for s in due("cell", step):
-                add_cell(s)
-            for s in due("product", step):
-                multiply_gates(s)
+                multiply_h(slot)
+                add_bias(slot)
+                if slot - QUANT_LAG in transposed_before:
+                    quantise_uh(transposed_before[slot - QUANT_LAG])
+            for what, (half, b) in due.get(slot, []):
+                if what == "tanh" and len(HALF_GROUPS[half]) == 1:
+                    epilogue(what, half, b)
+            if slot < STEPS:
+                squash(slot)
+            for kind in ("tanh", "ig", "fc", "cell", "out"):
+                for what, (half, b) in due.get(slot, []):
+                    if what == kind and not (what == "tanh" and len(HALF_GROUPS[half]) == 1):
+                        epilogue(what, half, b)

@@ -44,6 +44,7 @@ HALF_GATES = ((GATE_I, GATE_G, GATE_F, GATE_O), (GATE_I, GATE_G, GATE_F, GATE_O)
 HALF_GROUPS = (((0, 1, 2, 3, 4),), ((0,), (1,), (2,), (3,), (4,)))
 LEAD = 5
 QUANT_LAG = 1
+LAST_PIECES = 2
 
 FLOPS = 2 * BATCH * (2 * FEATURES) * (GATES * FEATURES)
 
@@ -245,6 +246,11 @@ def tile_lstmcell_e_kernel(tc, x_t, h_pre, c_pre, Wx_words, Wx_scales, bW, Uh, b
         sums = {}
         live = {}
 
+        def pieces(half, b):
+            parts = LAST_PIECES if (half, b) == (order[-1][0], order[-1][2]) else 1
+            width = N_TILE // parts
+            return [slice(width * part, width * (part + 1)) for part in range(parts)]
+
         def multiply_x(slot):
             half, gate, b = order[slot]
             if slot > last_transposes + 4 and slot % 2 == 1:
@@ -281,31 +287,43 @@ def tile_lstmcell_e_kernel(tc, x_t, h_pre, c_pre, Wx_words, Wx_scales, bW, Uh, b
             half, gate, b = order[slot]
             first = FEATURES * gate + N_TILE * half
             value = gates.tile([P, N_TILE], F32, tag="gate%d" % gate)
-            nc.vector.tensor_tensor(out=value[:], in0=sums[slot][:], in1=bias[:, first : first + N_TILE], op=ALU.add)
+            for part in pieces(half, b):
+                nc.vector.tensor_tensor(
+                    out=value[:, part], in0=sums[slot][:, part], in1=bias[:, first + part.start : first + part.stop], op=ALU.add
+                )
             live[(gate, half, b)] = value
 
         def squash(slot):
             half, gate, b = order[slot]
             value = live[(gate, half, b)]
-            nc.scalar.activation(out=value[:], in_=value[:], func=ACT.Tanh if gate == GATE_G else ACT.Sigmoid)
+            for part in pieces(half, b):
+                nc.scalar.activation(out=value[:, part], in_=value[:, part], func=ACT.Tanh if gate == GATE_G else ACT.Sigmoid)
 
         def epilogue(what, half, b):
-            cols = slice(N_TILE * half, N_TILE * (half + 1))
             rows = slice(P * b, P * (b + 1))
-            if what == "ig":
-                nc.gpsimd.tensor_tensor(out=live[(GATE_G, half, b)][:], in0=live[(GATE_G, half, b)][:], in1=live[(GATE_I, half, b)][:], op=ALU.mult)
-            if what == "fc":
-                nc.vector.tensor_tensor(out=live[(GATE_F, half, b)][:], in0=live[(GATE_F, half, b)][:], in1=c_old[:, b, cols], op=ALU.mult)
-            if what == "cell":
-                (nc.gpsimd if (half == HALVES - 1 and b != HALF_GROUPS[half][-1][-1]) else nc.vector).tensor_tensor(out=live[(GATE_F, half, b)][:], in0=live[(GATE_F, half, b)][:], in1=live[(GATE_G, half, b)][:], op=ALU.add)
-                nc.sync.dma_start(out=out_1[rows, cols], in_=live[(GATE_F, half, b)][:])
+            last_tile = (half, b) == (order[-1][0], order[-1][2])
+            tile_by_tile = len(HALF_GROUPS[half]) > 1
             if what == "tanh":
-                squashed = gates.tile([P, N_TILE], F32, tag="tanh")
-                nc.scalar.activation(out=squashed[:], in_=live[(GATE_F, half, b)][:], func=ACT.Tanh)
-                live[("tanh", half, b)] = squashed
-            if what == "out":
-                nc.vector.tensor_tensor(out=live[(GATE_O, half, b)][:], in0=live[(GATE_O, half, b)][:], in1=live[("tanh", half, b)][:], op=ALU.mult)
-                nc.sync.dma_start(out=out_0[rows, cols], in_=live[(GATE_O, half, b)][:])
+                live[("tanh", half, b)] = gates.tile([P, N_TILE], F32, tag="tanh", name="squashed")
+            for part in pieces(half, b):
+                cols = slice(N_TILE * half + part.start, N_TILE * half + part.stop)
+                if what == "ig":
+                    g_t = live[(GATE_G, half, b)][:, part]
+                    nc.gpsimd.tensor_tensor(out=g_t, in0=g_t, in1=live[(GATE_I, half, b)][:, part], op=ALU.mult)
+                if what == "fc":
+                    f_t = live[(GATE_F, half, b)][:, part]
+                    nc.vector.tensor_tensor(out=f_t, in0=f_t, in1=c_old[:, b, cols], op=ALU.mult)
+                if what == "cell":
+                    f_t = live[(GATE_F, half, b)][:, part]
+                    adder = nc.gpsimd if tile_by_tile and not last_tile else nc.vector
+                    adder.tensor_tensor(out=f_t, in0=f_t, in1=live[(GATE_G, half, b)][:, part], op=ALU.add)
+                    nc.sync.dma_start(out=out_1[rows, cols], in_=f_t)
+                if what == "tanh":
+                    nc.scalar.activation(out=live[("tanh", half, b)][:, part], in_=live[(GATE_F, half, b)][:, part], func=ACT.Tanh)
+                if what == "out":
+                    o_t = live[(GATE_O, half, b)][:, part]
+                    nc.vector.tensor_tensor(out=o_t, in0=o_t, in1=live[("tanh", half, b)][:, part], op=ALU.mult)
+                    nc.sync.dma_start(out=out_0[rows, cols], in_=o_t)
 
         loaded = [UH_RAW_BUFS]
 

@@ -226,11 +226,11 @@ def tile_lstmcell_e_kernel(tc, x_t, h_pre, c_pre, Wx_words, Wx_scales, bW, Uh, b
                 tile_by_tile = len(HALF_GROUPS[half]) > 1
                 on_pool = tile_by_tile and b != HALF_GROUPS[half][-1][-1]
                 if tile_by_tile:
-                    t_ig = max(s_i, s_g)
-                    t_fc = s_f + 1
-                    t_cell = t_fc
+                    t_ig = s_o
+                    t_fc = s_o
+                    t_cell = s_o
                     t_tanh = t_cell + (2 if on_pool else 1)
-                    t_out = t_cell + (6 if on_pool else 2)
+                    t_out = t_cell + (4 if on_pool else 2)
                 else:
                     t_ig = max(s_i, s_g) + PRODUCT_LAG
                     t_fc = s_f + PRODUCT_LAG
@@ -309,7 +309,7 @@ def tile_lstmcell_e_kernel(tc, x_t, h_pre, c_pre, Wx_words, Wx_scales, bW, Uh, b
                 cols = slice(N_TILE * half + part.start, N_TILE * half + part.stop)
                 if what == "ig":
                     g_t = live[(GATE_G, half, b)][:, part]
-                    nc.gpsimd.tensor_tensor(out=g_t, in0=g_t, in1=live[(GATE_I, half, b)][:, part], op=ALU.mult)
+                    (nc.vector if tile_by_tile else nc.gpsimd).tensor_tensor(out=g_t, in0=g_t, in1=live[(GATE_I, half, b)][:, part], op=ALU.mult)
                 if what == "fc":
                     f_t = live[(GATE_F, half, b)][:, part]
                     nc.vector.tensor_tensor(out=f_t, in0=f_t, in1=c_old[:, b, cols], op=ALU.mult)

@@ -33,6 +33,9 @@ CHUNKS = HALVES * GATES
 STEPS = CHUNKS * BATCH_TILES
 
 RUN = 2
+TILE_RUN = 2
+EARLY_X = 4
+ALTERNATE = False
 UH_RAW_BUFS = 4
 UH_CODE_BUFS = 6
 PRODUCT_LAG = 2
@@ -185,18 +188,15 @@ def tile_lstmcell_e_kernel(tc, x_t, h_pre, c_pre, Wx_words, Wx_scales, bW, Uh, b
 
         quantise_activations(x_raw, True, nc.vector.tensor_copy, x_codes, x_scales)
 
-        for j in range(GATES * HALVES):
-            cols = slice(N_TILE * j, N_TILE * (j + 1))
-            spread = z_banks.tile([P, N_TILE], F32, tag="z")
-            nc.tensor.matmul(out=spread[:], lhsT=ones[:], rhs=bias_rows[:, cols], start=True, stop=True)
-            if j % 2 == 0:
-                nc.scalar.copy(out=bias[:, cols], in_=spread[:])
-            else:
-                nc.vector.tensor_copy(out=bias[:, cols], in_=spread[:])
+        def spread_bias(half, copy):
+            for gate in range(GATES):
+                j = HALVES * gate + half
+                cols = slice(N_TILE * j, N_TILE * (j + 1))
+                spread = z_banks.tile([P, N_TILE], F32, tag="z")
+                nc.tensor.matmul(out=spread[:], lhsT=ones[:], rhs=bias_rows[:, cols], start=True, stop=True)
+                copy(out=bias[:, cols], in_=spread[:])
 
-        transpose_uh(0)
-        quantise_uh(0)
-        quantise_activations(h_raw, False, nc.scalar.copy, h_codes, h_scales)
+        spread_bias(0, nc.scalar.copy)
 
         order = []
         for half in range(HALVES):
@@ -251,12 +251,18 @@ def tile_lstmcell_e_kernel(tc, x_t, h_pre, c_pre, Wx_words, Wx_scales, bW, Uh, b
             width = N_TILE // parts
             return [slice(width * part, width * (part + 1)) for part in range(parts)]
 
-        def multiply_x(slot):
-            half, gate, b = order[slot]
+        def open_bank(slot):
             if slot > last_transposes + 4 and slot % 2 == 1:
                 z = t_banks.tile([P, N_TILE], F32, tag="bank")
             else:
                 z = z_banks.tile([P, N_TILE], F32, tag="z")
+            sums[slot] = z
+
+        def multiply_x(slot, opens):
+            half, gate, b = order[slot]
+            if opens:
+                open_bank(slot)
+            z = sums[slot]
             for g in range(PASSES):
                 nc.tensor.matmul_mx(
                     out=z[:],
@@ -264,14 +270,15 @@ def tile_lstmcell_e_kernel(tc, x_t, h_pre, c_pre, Wx_words, Wx_scales, bW, Uh, b
                     lhsT_scale=x_scales[:, b, g, :],
                     rhs=wx_words[:, PASSES * gate + g, 2 * N_TILE * half : 2 * N_TILE * (half + 1)].bitcast(FP4X4),
                     rhs_scale=wx_scales[:, PASSES * gate + g, N_TILE * half : N_TILE * (half + 1)],
-                    start=(g == 0),
-                    stop=False,
+                    start=(opens and g == 0),
+                    stop=(not opens and g == PASSES - 1),
                 )
-            sums[slot] = z
 
-        def multiply_h(slot):
+        def multiply_h(slot, opens):
             half, gate, b = order[slot]
             chunk = chunk_of(half, gate)
+            if opens:
+                open_bank(slot)
             for g in range(PASSES):
                 nc.tensor.matmul_mx(
                     out=sums[slot][:],
@@ -279,8 +286,8 @@ def tile_lstmcell_e_kernel(tc, x_t, h_pre, c_pre, Wx_words, Wx_scales, bW, Uh, b
                     lhsT_scale=h_scales[:, b, g, :],
                     rhs=uh_codes[chunk][:, g, :].bitcast(FP8X4),
                     rhs_scale=uh_scales[chunk][:, g, :],
-                    start=False,
-                    stop=(g == PASSES - 1),
+                    start=(opens and g == 0),
+                    stop=(not opens and g == PASSES - 1),
                 )
 
         def add_bias(slot):
@@ -326,18 +333,42 @@ def tile_lstmcell_e_kernel(tc, x_t, h_pre, c_pre, Wx_words, Wx_scales, bW, Uh, b
                     nc.sync.dma_start(out=out_0[rows, cols], in_=o_t)
 
         loaded = [UH_RAW_BUFS]
+        transpose_uh(0)
+        spread_bias(1, nc.vector.tensor_copy)
+        quantise_uh(0)
+        for early in range(EARLY_X // 2):
+            multiply_x(early, True)
+        quantise_activations(h_raw, False, nc.scalar.copy, h_codes, h_scales)
+        for early in range(EARLY_X // 2, EARLY_X):
+            multiply_x(early, True)
+        x_was_last = [True]
 
         for slot in range(STEPS + DRAIN):
             if slot < STEPS:
-                if slot % RUN == 0:
+                run = TILE_RUN if len(HALF_GROUPS[order[slot][0]]) > 1 else RUN
+                if slot % run == 0:
                     if slot in transposed_before:
                         transpose_uh(transposed_before[slot])
                         if loaded[0] < CHUNKS:
                             load_uh(loaded[0])
                             loaded[0] += 1
-                    for member in range(slot, min(slot + RUN, STEPS)):
-                        multiply_x(member)
-                multiply_h(slot)
+                    members = range(slot, min(slot + run, STEPS))
+                    if slot < EARLY_X:
+                        for member in members:
+                            multiply_h(member, False)
+                        x_was_last[0] = False
+                    elif x_was_last[0] or not ALTERNATE:
+                        for member in members:
+                            multiply_x(member, True)
+                        for member in members:
+                            multiply_h(member, False)
+                        x_was_last[0] = False
+                    else:
+                        for member in members:
+                            multiply_h(member, True)
+                        for member in members:
+                            multiply_x(member, False)
+                        x_was_last[0] = True
                 add_bias(slot)
                 if slot - QUANT_LAG in transposed_before:
                     quantise_uh(transposed_before[slot - QUANT_LAG])

@@ -77,7 +77,7 @@ def tile_lstmcell_e_kernel(tc, x_t, h_pre, c_pre, Wx_words, Wx_scales, bW, Uh, b
         x_scales = keep.tile([P, BATCH_TILES, PASSES, P], U8, align_bytes=64)
         h_codes = keep.tile([P, BATCH_TILES, PASSES, P], U32, align_bytes=64)
         h_scales = keep.tile([P, BATCH_TILES, PASSES, P], U8, align_bytes=64)
-        wx_words = keep.tile([P, GATES * PASSES, 2 * FEATURES], U8, align_bytes=64)
+        wx_words = keep.tile([P, HALVES, GATES * PASSES, 2 * N_TILE], U8, align_bytes=64)
         wx_scales = keep.tile([P, GATES * PASSES, FEATURES], U8, align_bytes=64)
 
         nc.vector.memset(bias_rows[:].bitcast(I32), 0)
@@ -95,11 +95,12 @@ def tile_lstmcell_e_kernel(tc, x_t, h_pre, c_pre, Wx_words, Wx_scales, bW, Uh, b
         def gate_of(chunk):
             return HALF_GATES[chunk // GATES][chunk % GATES]
 
-        def load_wx_words(gate):
+        def load_wx_words(gate, half=0):
             passes = slice(PASSES * gate, PASSES * (gate + 1))
+            part = slice(2 * N_TILE * half, 2 * N_TILE * (half + 1))
             nc.sync.dma_start(
-                out=wx_words[:, passes, :].bitcast(I32),
-                in_=Wx_words[passes].rearrange("j p w -> p j w").bitcast(I32),
+                out=wx_words[:, half, passes, :].bitcast(I32),
+                in_=Wx_words[passes, :, part].rearrange("j p w -> p j w").bitcast(I32),
             )
 
         uh_raw = {}
@@ -129,6 +130,8 @@ def tile_lstmcell_e_kernel(tc, x_t, h_pre, c_pre, Wx_words, Wx_scales, bW, Uh, b
                 nc.sync.dma_start(out=c_old[:], in_=c_pre.rearrange("(b p) n -> p b n", p=P))
             load_uh(chunk)
             load_wx_words(gate_of(chunk))
+        for chunk in range(GATES):
+            load_wx_words(gate_of(chunk), 1)
 
         def transpose_rows(rows, every_second_word):
             words = rows.bitcast(F32)
@@ -268,7 +271,7 @@ def tile_lstmcell_e_kernel(tc, x_t, h_pre, c_pre, Wx_words, Wx_scales, bW, Uh, b
                     out=z[:],
                     lhsT=x_codes[:, b, g, :].bitcast(FP8X4),
                     lhsT_scale=x_scales[:, b, g, :],
-                    rhs=wx_words[:, PASSES * gate + g, 2 * N_TILE * half : 2 * N_TILE * (half + 1)].bitcast(FP4X4),
+                    rhs=wx_words[:, half, PASSES * gate + g, :].bitcast(FP4X4),
                     rhs_scale=wx_scales[:, PASSES * gate + g, N_TILE * half : N_TILE * (half + 1)],
                     start=(opens and g == 0),
                     stop=(not opens and g == PASSES - 1),
@@ -329,7 +332,7 @@ def tile_lstmcell_e_kernel(tc, x_t, h_pre, c_pre, Wx_words, Wx_scales, bW, Uh, b
                     nc.scalar.activation(out=live[("tanh", half, b)][:, part], in_=live[(GATE_F, half, b)][:, part], func=ACT.Tanh)
                 if what == "out":
                     o_t = live[(GATE_O, half, b)][:, part]
-                    nc.vector.tensor_tensor(out=o_t, in0=o_t, in1=live[("tanh", half, b)][:, part], op=ALU.mult)
+                    (nc.gpsimd if tile_by_tile and b < BATCH_TILES - 2 else nc.vector).tensor_tensor(out=o_t, in0=o_t, in1=live[("tanh", half, b)][:, part], op=ALU.mult)
                     nc.sync.dma_start(out=out_0[rows, cols], in_=o_t)
 
         loaded = [UH_RAW_BUFS]

@@ -41,9 +41,10 @@ UH_CODE_BUFS = 6
 PRODUCT_LAG = 2
 CELL_LAG = 1
 TANH_LAG = 2
+FC_LAG = 6
 DRAIN = 8
 
-HALF_GATES = ((GATE_I, GATE_G, GATE_F, GATE_O), (GATE_I, GATE_G, GATE_F, GATE_O))
+HALF_GATES = ((GATE_F, GATE_I, GATE_G, GATE_O), (GATE_I, GATE_G, GATE_F, GATE_O))
 HALF_GROUPS = (((0, 1, 2, 3, 4),), ((0,), (1,), (2,), (3,), (4,)))
 LEAD = 5
 QUANT_LAG = 1
@@ -103,32 +104,40 @@ def tile_lstmcell_e_kernel(tc, x_t, h_pre, c_pre, Wx_words, Wx_scales, bW, Uh, b
                 in_=Wx_words[passes, :, part].rearrange("j p w -> p j w").bitcast(I32),
             )
 
+        def load_wx_scales(first, last):
+            for q in range(4):
+                nc.sync.dma_start(
+                    out=wx_scales[32 * q : 32 * q + 4, first:last, :].bitcast(I32),
+                    in_=Wx_scales[first:last, 4 * q : 4 * (q + 1), :].rearrange("j q n -> q j n").bitcast(I32),
+                )
+
         uh_raw = {}
 
-        def load_uh(chunk):
+        def load_uh(chunk, parts=1):
             half, gate = chunk // GATES, gate_of(chunk)
             raw = uh_raw_pool.tile([P, ROW_TILES, FEATURES], BF16)
-            nc.sync.dma_start(
-                out=raw[:],
-                in_=Uh[gate, N_TILE * half : N_TILE * (half + 1), :].rearrange("(r p) k -> p r k", p=P),
-            )
+            rows = ROW_TILES // parts
+            for part in range(parts):
+                first = N_TILE * half + P * rows * part
+                nc.sync.dma_start(
+                    out=raw[:, rows * part : rows * (part + 1), :],
+                    in_=Uh[gate, first : first + P * rows, :].rearrange("(r p) k -> p r k", p=P),
+                )
             uh_raw[chunk] = raw
 
         for b in range(BATCH_TILES):
             nc.sync.dma_start(out=x_raw[:, b, :], in_=x_t[P * b : P * (b + 1), :])
-        load_uh(0)
-        for q in range(8):
-            nc.sync.dma_start(
-                out=wx_scales[32 * (q // 4) + q % 4 : P : 64].bitcast(I32),
-                in_=Wx_scales[:, q : 16 : 8, :].rearrange("j q n -> q j n").bitcast(I32),
-            )
+        load_uh(0, 2)
+        load_wx_scales(0, 4)
         load_wx_words(gate_of(0))
         for b in range(BATCH_TILES):
             nc.sync.dma_start(out=h_raw[:, b, :], in_=h_pre[P * b : P * (b + 1), :])
         for chunk in range(1, GATES):
-            if gate_of(chunk - 1) == GATE_F:
+            if chunk == 3:
                 nc.sync.dma_start(out=c_old[:], in_=c_pre.rearrange("(b p) n -> p b n", p=P))
             load_uh(chunk)
+            if chunk == 2:
+                load_wx_scales(4, 8)
             load_wx_words(gate_of(chunk))
         for chunk in range(GATES):
             load_wx_words(gate_of(chunk), 1)
@@ -229,14 +238,14 @@ def tile_lstmcell_e_kernel(tc, x_t, h_pre, c_pre, Wx_words, Wx_scales, bW, Uh, b
                 tile_by_tile = len(HALF_GROUPS[half]) > 1
                 on_pool = tile_by_tile and b != HALF_GROUPS[half][-1][-1]
                 if tile_by_tile:
-                    t_ig = s_o
+                    t_ig = s_o if on_pool else s_f
                     t_fc = s_o
                     t_cell = s_o
                     t_tanh = t_cell + (2 if on_pool else 1)
                     t_out = t_cell + (4 if on_pool else 2)
                 else:
                     t_ig = max(s_i, s_g) + PRODUCT_LAG
-                    t_fc = s_f + PRODUCT_LAG
+                    t_fc = s_f + FC_LAG
                     t_cell = max(t_ig, t_fc) + CELL_LAG
                     t_tanh = t_cell + TANH_LAG
                     t_out = max(t_tanh + 1, s_o + PRODUCT_LAG)
@@ -348,7 +357,7 @@ def tile_lstmcell_e_kernel(tc, x_t, h_pre, c_pre, Wx_words, Wx_scales, bW, Uh, b
 
         for slot in range(STEPS + DRAIN):
             if slot < STEPS:
-                run = TILE_RUN if len(HALF_GROUPS[order[slot][0]]) > 1 else RUN
+                run = 1 if slot >= STEPS - 2 else TILE_RUN if len(HALF_GROUPS[order[slot][0]]) > 1 else RUN
                 if slot % run == 0:
                     if slot in transposed_before:
                         transpose_uh(transposed_before[slot])

@@ -105,10 +105,10 @@ def tile_lstmcell_e_kernel(tc, x_t, h_pre, c_pre, Wx_words, Wx_scales, bW, Uh, b
             )
 
         def load_wx_scales(first, last):
-            for q in range(4):
+            for q in range(8):
                 nc.sync.dma_start(
-                    out=wx_scales[32 * q : 32 * q + 4, first:last, :].bitcast(I32),
-                    in_=Wx_scales[first:last, 4 * q : 4 * (q + 1), :].rearrange("j q n -> q j n").bitcast(I32),
+                    out=wx_scales[32 * (q // 4) + q % 4 : P : 64, first:last, :].bitcast(I32),
+                    in_=Wx_scales[first:last, q : 16 : 8, :].rearrange("j q n -> q j n").bitcast(I32),
                 )
 
         uh_raw = {}
@@ -128,7 +128,7 @@ def tile_lstmcell_e_kernel(tc, x_t, h_pre, c_pre, Wx_words, Wx_scales, bW, Uh, b
         for b in range(BATCH_TILES):
             nc.sync.dma_start(out=x_raw[:, b, :], in_=x_t[P * b : P * (b + 1), :])
         load_uh(0, 2)
-        load_wx_scales(0, 4)
+        load_wx_scales(0, 8)
         load_wx_words(gate_of(0))
         for b in range(BATCH_TILES):
             nc.sync.dma_start(out=h_raw[:, b, :], in_=h_pre[P * b : P * (b + 1), :])
@@ -136,8 +136,6 @@ def tile_lstmcell_e_kernel(tc, x_t, h_pre, c_pre, Wx_words, Wx_scales, bW, Uh, b
             if chunk == 3:
                 nc.sync.dma_start(out=c_old[:], in_=c_pre.rearrange("(b p) n -> p b n", p=P))
             load_uh(chunk)
-            if chunk == 2:
-                load_wx_scales(4, 8)
             load_wx_words(gate_of(chunk))
         for chunk in range(GATES):
             load_wx_words(gate_of(chunk), 1)

@@ -46,7 +46,7 @@ DRAIN = 8
 
 HALF_GATES = ((GATE_F, GATE_I, GATE_G, GATE_O), (GATE_I, GATE_G, GATE_F, GATE_O))
 HALF_GROUPS = (((0, 1, 2, 3, 4),), ((0,), (1,), (2,), (3,), (4,)))
-LEAD = 5
+LEAD = 7
 QUANT_LAG = 1
 LAST_PIECES = 2
 
@@ -132,13 +132,12 @@ def tile_lstmcell_e_kernel(tc, x_t, h_pre, c_pre, Wx_words, Wx_scales, bW, Uh, b
         load_wx_words(gate_of(0))
         for b in range(BATCH_TILES):
             nc.sync.dma_start(out=h_raw[:, b, :], in_=h_pre[P * b : P * (b + 1), :])
-        for chunk in range(1, GATES):
-            if chunk == 3:
-                nc.sync.dma_start(out=c_old[:], in_=c_pre.rearrange("(b p) n -> p b n", p=P))
-            load_uh(chunk)
-            load_wx_words(gate_of(chunk))
-        for chunk in range(GATES):
-            load_wx_words(gate_of(chunk), 1)
+        load_uh(1)
+        load_wx_words(gate_of(1))
+        load_uh(2)
+        load_wx_words(gate_of(2))
+        load_uh(3)
+        load_wx_words(gate_of(3))
 
         def transpose_rows(rows, every_second_word):
             words = rows.bitcast(F32)
@@ -218,7 +217,7 @@ def tile_lstmcell_e_kernel(tc, x_t, h_pre, c_pre, Wx_words, Wx_scales, bW, Uh, b
             first_use.setdefault(chunk_of(half, gate), slot)
         transposed_before = {}
         for chunk in range(CHUNKS - 1, 0, -1):
-            slot = max(RUN, first_use[chunk] - LEAD)
+            slot = max(RUN * chunk, first_use[chunk] - LEAD)
             slot -= slot % RUN
             while slot in transposed_before:
                 slot -= RUN
@@ -236,7 +235,7 @@ def tile_lstmcell_e_kernel(tc, x_t, h_pre, c_pre, Wx_words, Wx_scales, bW, Uh, b
                 tile_by_tile = len(HALF_GROUPS[half]) > 1
                 on_pool = tile_by_tile and b != HALF_GROUPS[half][-1][-1]
                 if tile_by_tile:
-                    t_ig = s_o if on_pool else s_f
+                    t_ig = s_o
                     t_fc = s_o
                     t_cell = s_o
                     t_tanh = t_cell + (2 if on_pool else 1)
@@ -246,7 +245,7 @@ def tile_lstmcell_e_kernel(tc, x_t, h_pre, c_pre, Wx_words, Wx_scales, bW, Uh, b
                     t_fc = s_f + FC_LAG
                     t_cell = max(t_ig, t_fc) + CELL_LAG
                     t_tanh = t_cell + TANH_LAG
-                    t_out = max(t_tanh + 1, s_o + PRODUCT_LAG)
+                    t_out = max(t_tanh + 1, s_o + 3)
                 at(t_ig, "ig", (half, b))
                 at(t_fc, "fc", (half, b))
                 at(t_cell, "cell", (half, b))
@@ -339,11 +338,12 @@ def tile_lstmcell_e_kernel(tc, x_t, h_pre, c_pre, Wx_words, Wx_scales, bW, Uh, b
                     nc.scalar.activation(out=live[("tanh", half, b)][:, part], in_=live[(GATE_F, half, b)][:, part], func=ACT.Tanh)
                 if what == "out":
                     o_t = live[(GATE_O, half, b)][:, part]
-                    (nc.gpsimd if tile_by_tile and b < BATCH_TILES - 2 else nc.vector).tensor_tensor(out=o_t, in0=o_t, in1=live[("tanh", half, b)][:, part], op=ALU.mult)
+                    (nc.gpsimd if (b < BATCH_TILES - 2 if tile_by_tile else 2 <= b < 5) else nc.vector).tensor_tensor(out=o_t, in0=o_t, in1=live[("tanh", half, b)][:, part], op=ALU.mult)
                     nc.sync.dma_start(out=out_0[rows, cols], in_=o_t)
 
-        loaded = [UH_RAW_BUFS]
         transpose_uh(0)
+        nc.sync.dma_start(out=c_old[:], in_=c_pre.rearrange("(b p) n -> p b n", p=P))
+        load_uh(UH_RAW_BUFS)
         spread_bias(1, nc.vector.tensor_copy)
         quantise_uh(0)
         for early in range(EARLY_X // 2):
@@ -355,13 +355,15 @@ def tile_lstmcell_e_kernel(tc, x_t, h_pre, c_pre, Wx_words, Wx_scales, bW, Uh, b
 
         for slot in range(STEPS + DRAIN):
             if slot < STEPS:
-                run = 1 if slot >= STEPS - 2 else TILE_RUN if len(HALF_GROUPS[order[slot][0]]) > 1 else RUN
+                run = TILE_RUN if len(HALF_GROUPS[order[slot][0]]) > 1 else RUN
                 if slot % run == 0:
                     if slot in transposed_before:
                         transpose_uh(transposed_before[slot])
-                        if loaded[0] < CHUNKS:
-                            load_uh(loaded[0])
-                            loaded[0] += 1
+                        behind = transposed_before[slot] + UH_RAW_BUFS
+                        if behind < CHUNKS:
+                            load_uh(behind)
+                        if behind - 1 < CHUNKS:
+                            load_wx_words(gate_of(behind - 1), 1)
                     members = range(slot, min(slot + run, STEPS))
                     if slot < EARLY_X:
                         for member in members:

@@ -125,13 +125,16 @@ def tile_lstmcell_e_kernel(tc, x_t, h_pre, c_pre, Wx_words, Wx_scales, bW, Uh, b
                 )
             uh_raw[chunk] = raw
 
-        for b in range(BATCH_TILES):
-            nc.sync.dma_start(out=x_raw[:, b, :], in_=x_t[P * b : P * (b + 1), :])
+        def by_tile(rows):
+            return rows.rearrange("(p b) n -> p b n", b=BATCH_TILES)
+
+        for first, last in ((0,1),(1,3),(3,5)):
+            nc.sync.dma_start(out=x_raw[:, first:last, :], in_=by_tile(x_t)[:, first:last, :])
         load_uh(0, 2)
         load_wx_scales(0, 8)
         load_wx_words(gate_of(0))
-        for b in range(BATCH_TILES):
-            nc.sync.dma_start(out=h_raw[:, b, :], in_=h_pre[P * b : P * (b + 1), :])
+        for first, last in ((0,1),(1,3),(3,5)):
+            nc.sync.dma_start(out=h_raw[:, first:last, :], in_=by_tile(h_pre)[:, first:last, :])
         load_uh(1)
         load_wx_words(gate_of(1))
         load_uh(2)
@@ -316,7 +319,6 @@ def tile_lstmcell_e_kernel(tc, x_t, h_pre, c_pre, Wx_words, Wx_scales, bW, Uh, b
                 nc.scalar.activation(out=value[:, part], in_=value[:, part], func=ACT.Tanh if gate == GATE_G else ACT.Sigmoid)
 
         def epilogue(what, half, b):
-            rows = slice(P * b, P * (b + 1))
             last_tile = (half, b) == (order[-1][0], order[-1][2])
             tile_by_tile = len(HALF_GROUPS[half]) > 1
             if what == "tanh":
@@ -333,16 +335,16 @@ def tile_lstmcell_e_kernel(tc, x_t, h_pre, c_pre, Wx_words, Wx_scales, bW, Uh, b
                     f_t = live[(GATE_F, half, b)][:, part]
                     adder = nc.gpsimd if tile_by_tile and not last_tile else nc.vector
                     adder.tensor_tensor(out=f_t, in0=f_t, in1=live[(GATE_G, half, b)][:, part], op=ALU.add)
-                    nc.sync.dma_start(out=out_1[rows, cols], in_=f_t)
+                    nc.sync.dma_start(out=by_tile(out_1)[:, b, cols], in_=f_t)
                 if what == "tanh":
                     nc.scalar.activation(out=live[("tanh", half, b)][:, part], in_=live[(GATE_F, half, b)][:, part], func=ACT.Tanh)
                 if what == "out":
                     o_t = live[(GATE_O, half, b)][:, part]
                     (nc.gpsimd if (b < BATCH_TILES - 2 if tile_by_tile else 2 <= b < 5) else nc.vector).tensor_tensor(out=o_t, in0=o_t, in1=live[("tanh", half, b)][:, part], op=ALU.mult)
-                    nc.sync.dma_start(out=out_0[rows, cols], in_=o_t)
+                    nc.sync.dma_start(out=by_tile(out_0)[:, b, cols], in_=o_t)
 
         transpose_uh(0)
-        nc.sync.dma_start(out=c_old[:], in_=c_pre.rearrange("(b p) n -> p b n", p=P))
+        nc.sync.dma_start(out=c_old[:], in_=by_tile(c_pre))
         load_uh(UH_RAW_BUFS)
         spread_bias(1, nc.vector.tensor_copy)
         quantise_uh(0)

@@ -26,7 +26,8 @@ PASSES = FEATURES // K_PASS
 N_TILE = 512
 HALVES = FEATURES // N_TILE
 BATCH_TILES = BATCH // P
-ROW_TILES = N_TILE // P
+PAIR = 2
+ROW_BLOCKS = N_TILE // (PAIR * P)
 PASS_WORDS = K_PASS // 2
 
 CHUNKS = HALVES * GATES
@@ -115,13 +116,13 @@ def tile_lstmcell_e_kernel(tc, x_t, h_pre, c_pre, Wx_words, Wx_scales, bW, Uh, b
 
         def load_uh(chunk, parts=1):
             half, gate = chunk // GATES, gate_of(chunk)
-            raw = uh_raw_pool.tile([P, ROW_TILES, FEATURES], BF16)
-            rows = ROW_TILES // parts
+            raw = uh_raw_pool.tile([P, ROW_BLOCKS, PAIR, FEATURES], BF16)
+            blocks = ROW_BLOCKS // parts
             for part in range(parts):
-                first = N_TILE * half + P * rows * part
+                first = N_TILE * half + PAIR * P * blocks * part
                 nc.sync.dma_start(
-                    out=raw[:, rows * part : rows * (part + 1), :],
-                    in_=Uh[gate, first : first + P * rows, :].rearrange("(r p) k -> p r k", p=P),
+                    out=raw[:, blocks * part : blocks * (part + 1)],
+                    in_=Uh[gate, first : first + PAIR * P * blocks, :].rearrange("(q p e) k -> p q e k", p=P, e=PAIR),
                 )
             uh_raw[chunk] = raw
 
@@ -182,9 +183,18 @@ def tile_lstmcell_e_kernel(tc, x_t, h_pre, c_pre, Wx_words, Wx_scales, bW, Uh, b
         def transpose_uh(chunk):
             four_k = uh_pool.tile([P, 4 * PASSES * N_TILE], BF16, align_bytes=64)
             slots = four_k[:].bitcast(F32).rearrange("p (g n u) -> p g n u", g=PASSES, u=2)
-            for r in range(ROW_TILES):
-                bank = transpose_rows(uh_raw[chunk][:, r, :], False)
-                nc.scalar.copy(out=slots[:, :, P * r : P * (r + 1), :], in_=side_by_side(bank))
+            for q in range(ROW_BLOCKS):
+                for g in range(PASSES):
+                    bank = t_banks.tile([P, 2 * PAIR, P], F32, tag="bank")
+                    for e in range(PAIR):
+                        words = uh_raw[chunk][:, q, e, :].bitcast(F32)
+                        for u in range(2):
+                            first = PASS_WORDS * g + P * u
+                            nc.tensor.transpose(bank[:, 2 * e + u, :], words[:, first : first + P], identity[:])
+                    nc.scalar.copy(
+                        out=slots[:, g, PAIR * P * q : PAIR * P * (q + 1), :].rearrange("p (c e) u -> p c e u", e=PAIR),
+                        in_=bank[:].rearrange("p (e u) c -> p c e u", e=PAIR),
+                    )
             uh_grouped[chunk] = four_k
 
         def quantise_uh(chunk):

@@ -191,7 +191,8 @@ def tile_lstmcell_e_kernel(tc, x_t, h_pre, c_pre, Wx_words, Wx_scales, bW, Uh, b
                         for u in range(2):
                             first = PASS_WORDS * g + P * u
                             nc.tensor.transpose(bank[:, 2 * e + u, :], words[:, first : first + P], identity[:])
-                    nc.scalar.copy(
+                    mover = nc.vector.tensor_copy if chunk < GATES and q == 0 else nc.scalar.copy
+                    mover(
                         out=slots[:, g, PAIR * P * q : PAIR * P * (q + 1), :].rearrange("p (c e) u -> p c e u", e=PAIR),
                         in_=bank[:].rearrange("p (e u) c -> p c e u", e=PAIR),
                     )
@@ -258,7 +259,7 @@ def tile_lstmcell_e_kernel(tc, x_t, h_pre, c_pre, Wx_words, Wx_scales, bW, Uh, b
                     t_fc = s_f + FC_LAG
                     t_cell = max(t_ig, t_fc) + CELL_LAG
                     t_tanh = t_cell + TANH_LAG
-                    t_out = max(t_tanh + 1, s_o + 3)
+                    t_out = max(t_tanh + 1, s_o + 2)
                 at(t_ig, "ig", (half, b))
                 at(t_fc, "fc", (half, b))
                 at(t_cell, "cell", (half, b))
@@ -340,7 +341,7 @@ def tile_lstmcell_e_kernel(tc, x_t, h_pre, c_pre, Wx_words, Wx_scales, bW, Uh, b
                     (nc.vector if tile_by_tile else nc.gpsimd).tensor_tensor(out=g_t, in0=g_t, in1=live[(GATE_I, half, b)][:, part], op=ALU.mult)
                 if what == "fc":
                     f_t = live[(GATE_F, half, b)][:, part]
-                    nc.vector.tensor_tensor(out=f_t, in0=f_t, in1=c_old[:, b, cols], op=ALU.mult)
+                    (nc.vector if tile_by_tile else nc.gpsimd).tensor_tensor(out=f_t, in0=f_t, in1=c_old[:, b, cols], op=ALU.mult)
                 if what == "cell":
                     f_t = live[(GATE_F, half, b)][:, part]
                     adder = nc.gpsimd if tile_by_tile and not last_tile else nc.vector
@@ -350,7 +351,7 @@ def tile_lstmcell_e_kernel(tc, x_t, h_pre, c_pre, Wx_words, Wx_scales, bW, Uh, b
                     nc.scalar.activation(out=live[("tanh", half, b)][:, part], in_=live[(GATE_F, half, b)][:, part], func=ACT.Tanh)
                 if what == "out":
                     o_t = live[(GATE_O, half, b)][:, part]
-                    (nc.gpsimd if (b < BATCH_TILES - 2 if tile_by_tile else 2 <= b < 5) else nc.vector).tensor_tensor(out=o_t, in0=o_t, in1=live[("tanh", half, b)][:, part], op=ALU.mult)
+                    (nc.gpsimd if (b < BATCH_TILES - 2 if tile_by_tile else 3 <= b < 5) else nc.vector).tensor_tensor(out=o_t, in0=o_t, in1=live[("tanh", half, b)][:, part], op=ALU.mult)
                     nc.sync.dma_start(out=by_tile(out_0)[:, b, cols], in_=o_t)
 
         transpose_uh(0)

from contextlib import ExitStack

import concourse.mybir as mybir
from concourse.masks import make_identity

F32 = mybir.dt.float32
BF16 = mybir.dt.bfloat16
I32 = mybir.dt.int32
U32 = mybir.dt.uint32
U8 = mybir.dt.uint8
FP8X4 = mybir.dt.float8_e4m3fn_x4
FP4X4 = mybir.dt.float4_e2m1fn_x4
ACT = mybir.ActivationFunctionType
ALU = mybir.AluOpType

P = 128
BATCH = 640
FEATURES = 1024
GATES = 4
GATE_F = 0
GATE_I = 1
GATE_O = 2
GATE_G = 3
K_PASS = 512
PASSES = FEATURES // K_PASS
N_TILE = 512
HALVES = FEATURES // N_TILE
BATCH_TILES = BATCH // P
PAIR = 2
ROW_BLOCKS = N_TILE // (PAIR * P)
PASS_WORDS = K_PASS // 2

CHUNKS = HALVES * GATES
STEPS = CHUNKS * BATCH_TILES

RUN = 2
TILE_RUN = 2
EARLY_X = 4
ALTERNATE = False
UH_RAW_BUFS = 4
UH_CODE_BUFS = 6
PRODUCT_LAG = 2
CELL_LAG = 1
TANH_LAG = 2
FC_LAG = 6
DRAIN = 8

HALF_GATES = ((GATE_F, GATE_I, GATE_G, GATE_O), (GATE_I, GATE_G, GATE_F, GATE_O))
HALF_GROUPS = (((0, 1, 2, 3, 4),), ((0,), (1,), (2,), (3,), (4,)))
LEAD = 7
QUANT_LAG = 1
LAST_PIECES = 2

FLOPS = 2 * BATCH * (2 * FEATURES) * (GATES * FEATURES)


def tile_lstmcell_e_kernel(tc, x_t, h_pre, c_pre, Wx_words, Wx_scales, bW, Uh, bU, out_0, out_1):
    nc = tc.nc
    with ExitStack() as ctx:
        keep = ctx.enter_context(tc.tile_pool(name="keep", bufs=1))
        stage = ctx.enter_context(tc.tile_pool(name="stage", bufs=3))
        uh_raw_pool = ctx.enter_context(tc.tile_pool(name="uh_raw", bufs=UH_RAW_BUFS))
        uh_pool = ctx.enter_context(tc.tile_pool(name="uh", bufs=2))
        uh_code_pool = ctx.enter_context(tc.tile_pool(name="uh_code", bufs=UH_CODE_BUFS))
        gates = ctx.enter_context(tc.tile_pool(name="gates", bufs=BATCH_TILES))
        z_banks = ctx.enter_context(tc.psum_pool(name="z_banks", bufs=4))
        t_banks = ctx.enter_context(tc.psum_pool(name="t_banks", bufs=4))
        ctx.enter_context(tc.manual_schedule())

        identity = keep.tile([P, P], F32)
        ones = keep.tile([P, P], BF16)
        table_warmer = keep.tile([P, 1], F32)
        bias_rows = keep.tile([P, GATES * FEATURES], BF16)
        bias = keep.tile([P, GATES * FEATURES], F32)
        x_raw = keep.tile([P, BATCH_TILES, FEATURES], BF16)
        h_raw = keep.tile([P, BATCH_TILES, FEATURES], BF16)
        c_old = keep.tile([P, BATCH_TILES, FEATURES], BF16)
        x_codes = keep.tile([P, BATCH_TILES, PASSES, P], U32, align_bytes=64)
        x_scales = keep.tile([P, BATCH_TILES, PASSES, P], U8, align_bytes=64)
        h_codes = keep.tile([P, BATCH_TILES, PASSES, P], U32, align_bytes=64)
        h_scales = keep.tile([P, BATCH_TILES, PASSES, P], U8, align_bytes=64)
        wx_words = keep.tile([P, HALVES, GATES * PASSES, 2 * N_TILE], U8, align_bytes=64)
        wx_scales = keep.tile([P, GATES * PASSES, FEATURES], U8, align_bytes=64)

        nc.vector.memset(bias_rows[:].bitcast(I32), 0)
        nc.scalar.dma_start(out=bias_rows[0:1, :], in_=bW.rearrange("(o g) n -> o (g n)", o=1))
        nc.scalar.dma_start(out=bias_rows[1:2, :], in_=bU.rearrange("(o g) n -> o (g n)", o=1))
        nc.vector.memset(table_warmer[:], 0.0)
        nc.scalar.activation(out=table_warmer[:], in_=table_warmer[:], func=ACT.Sigmoid)
        nc.vector.memset(wx_scales[:].rearrange("p j n -> p (j n)").bitcast(I32), 0)
        make_identity(nc, identity[:])
        nc.gpsimd.memset(ones[:], 1.0)

        def chunk_of(half, gate):
            return GATES * half + HALF_GATES[half].index(gate)

        def gate_of(chunk):
            return HALF_GATES[chunk // GATES][chunk % GATES]

        def load_wx_words(gate, half=0):
            passes = slice(PASSES * gate, PASSES * (gate + 1))
            part = slice(2 * N_TILE * half, 2 * N_TILE * (half + 1))
            nc.sync.dma_start(
                out=wx_words[:, half, passes, :].bitcast(I32),
                in_=Wx_words[passes, :, part].rearrange("j p w -> p j w").bitcast(I32),
            )

        def load_wx_scales(first, last):
            for q in range(8):
                nc.sync.dma_start(
                    out=wx_scales[32 * (q // 4) + q % 4 : P : 64, first:last, :].bitcast(I32),
                    in_=Wx_scales[first:last, q : 16 : 8, :].rearrange("j q n -> q j n").bitcast(I32),
                )

        uh_raw = {}

        def load_uh(chunk, parts=1):
            half, gate = chunk // GATES, gate_of(chunk)
            raw = uh_raw_pool.tile([P, ROW_BLOCKS, PAIR, FEATURES], BF16)
            blocks = ROW_BLOCKS // parts
            for part in range(parts):
                first = N_TILE * half + PAIR * P * blocks * part
                nc.sync.dma_start(
                    out=raw[:, blocks * part : blocks * (part + 1)],
                    in_=Uh[gate, first : first + PAIR * P * blocks, :].rearrange("(q p e) k -> p q e k", p=P, e=PAIR),
                )
            uh_raw[chunk] = raw

        def by_tile(rows):
            return rows.rearrange("(p b) n -> p b n", b=BATCH_TILES)

        for first, last in ((0,1),(1,3),(3,5)):
            nc.sync.dma_start(out=x_raw[:, first:last, :], in_=by_tile(x_t)[:, first:last, :])
        load_uh(0, 2)
        load_wx_scales(0, 8)
        load_wx_words(gate_of(0))
        for first, last in ((0,1),(1,3),(3,5)):
            nc.sync.dma_start(out=h_raw[:, first:last, :], in_=by_tile(h_pre)[:, first:last, :])
        load_uh(1)
        load_wx_words(gate_of(1))
        load_uh(2)
        load_wx_words(gate_of(2))
        load_uh(3)
        load_wx_words(gate_of(3))

        def transpose_rows(rows, every_second_word):
            words = rows.bitcast(F32)
            bank = t_banks.tile([P, 2 * PASSES, P], F32, tag="bank")
            for g in range(PASSES):
                for u in range(2):
                    if every_second_word:
                        cols = words[:, PASS_WORDS * g + u : PASS_WORDS * (g + 1) : 2]
                    else:
                        cols = words[:, PASS_WORDS * g + P * u : PASS_WORDS * g + P * (u + 1)]
                    nc.tensor.transpose(bank[:, 2 * g + u, :], cols, identity[:])
            return bank

        def side_by_side(bank):
            return bank[:].rearrange("p (g u) r -> p g r u", u=2)

        def quantise_activations(raw, every_second_word, copy, codes, scales):
            grouped = {}
            for b in range(BATCH_TILES + 1):
                if b < BATCH_TILES:
                    bank = transpose_rows(raw[:, b, :], every_second_word)
                    four_k = stage.tile([P, 4 * PASSES * P], BF16, align_bytes=64)
                    copy(
                        out=four_k[:].bitcast(F32).rearrange("p (g r u) -> p g r u", g=PASSES, u=2),
                        in_=side_by_side(bank),
                    )
                    grouped[b] = four_k
                if b > 0:
                    nc.vector.quantize_mx(
                        out=codes[:, b - 1].rearrange("p g r -> p (g r)").bitcast(FP8X4),
                        scales=scales[:, b - 1].rearrange("p g r -> p (g r)"),
                        in_=grouped[b - 1][:],
                    )

        uh_grouped = {}
        uh_codes = {}
        uh_scales = {}

        def transpose_uh(chunk):
            four_k = uh_pool.tile([P, 4 * PASSES * N_TILE], BF16, align_bytes=64)
            slots = four_k[:].bitcast(F32).rearrange("p (g n u) -> p g n u", g=PASSES, u=2)
            for q in range(ROW_BLOCKS):
                for g in range(PASSES):
                    bank = t_banks.tile([P, 2 * PAIR, P], F32, tag="bank")
                    for e in range(PAIR):
                        words = uh_raw[chunk][:, q, e, :].bitcast(F32)
                        for u in range(2):
                            first = PASS_WORDS * g + P * u
                            nc.tensor.transpose(bank[:, 2 * e + u, :], words[:, first : first + P], identity[:])
                    mover = nc.vector.tensor_copy if chunk < GATES and q == 0 else nc.scalar.copy
                    mover(
                        out=slots[:, g, PAIR * P * q : PAIR * P * (q + 1), :].rearrange("p (c e) u -> p c e u", e=PAIR),
                        in_=bank[:].rearrange("p (e u) c -> p c e u", e=PAIR),
                    )
            uh_grouped[chunk] = four_k

        def quantise_uh(chunk):
            codes = uh_code_pool.tile([P, PASSES, N_TILE], U32, align_bytes=64)
            scales = uh_code_pool.tile([P, PASSES, N_TILE], U8, align_bytes=64)
            nc.vector.quantize_mx(
                out=codes[:].rearrange("p g n -> p (g n)").bitcast(FP8X4),
                scales=scales[:].rearrange("p g n -> p (g n)"),
                in_=uh_grouped[chunk][:],
            )
            uh_codes[chunk] = codes
            uh_scales[chunk] = scales

        quantise_activations(x_raw, True, nc.vector.tensor_copy, x_codes, x_scales)

        def spread_bias(half, copy):
            for gate in range(GATES):
                j = HALVES * gate + half
                cols = slice(N_TILE * j, N_TILE * (j + 1))
                spread = z_banks.tile([P, N_TILE], F32, tag="z")
                nc.tensor.matmul(out=spread[:], lhsT=ones[:], rhs=bias_rows[:, cols], start=True, stop=True)
                copy(out=bias[:, cols], in_=spread[:])

        spread_bias(0, nc.scalar.copy)

        order = []
        for half in range(HALVES):
            for group in HALF_GROUPS[half]:
                order.extend((half, gate, b) for gate in HALF_GATES[half] for b in group)
        slot_of = dict((place, slot) for slot, place in enumerate(order))
        first_use = {}
        for slot, (half, gate, b) in enumerate(order):
            first_use.setdefault(chunk_of(half, gate), slot)
        transposed_before = {}
        for chunk in range(CHUNKS - 1, 0, -1):
            slot = max(RUN * chunk, first_use[chunk] - LEAD)
            slot -= slot % RUN
            while slot in transposed_before:
                slot -= RUN
            transposed_before[slot] = chunk
        last_transposes = max(transposed_before)

        due = {}

        def at(slot, what, place):
            due.setdefault(slot, []).append((what, place))

        for half in range(HALVES):
            for b in range(BATCH_TILES):
                s_i, s_g, s_f, s_o = (slot_of[(half, gate, b)] for gate in (GATE_I, GATE_G, GATE_F, GATE_O))
                tile_by_tile = len(HALF_GROUPS[half]) > 1
                on_pool = tile_by_tile and b != HALF_GROUPS[half][-1][-1]
                if tile_by_tile:
                    t_ig = s_o
                    t_fc = s_o
                    t_cell = s_o
                    t_tanh = t_cell + (2 if on_pool else 1)
                    t_out = t_cell + (4 if on_pool else 2)
                else:
                    t_ig = max(s_i, s_g) + PRODUCT_LAG
                    t_fc = s_f + FC_LAG
                    t_cell = max(t_ig, t_fc) + CELL_LAG
                    t_tanh = t_cell + TANH_LAG
                    t_out = max(t_tanh + 1, s_o + 2)
                at(t_ig, "ig", (half, b))
                at(t_fc, "fc", (half, b))
                at(t_cell, "cell", (half, b))
                at(t_tanh, "tanh", (half, b))
                at(t_out, "out", (half, b))

        sums = {}
        live = {}

        def pieces(half, b):
            parts = LAST_PIECES if (half, b) == (order[-1][0], order[-1][2]) else 1
            width = N_TILE // parts
            return [slice(width * part, width * (part + 1)) for part in range(parts)]

        def open_bank(slot):
            if slot > last_transposes + 4 and slot % 2 == 1:
                z = t_banks.tile([P, N_TILE], F32, tag="bank")
            else:
                z = z_banks.tile([P, N_TILE], F32, tag="z")
            sums[slot] = z

        def multiply_x(slot, opens):
            half, gate, b = order[slot]
            if opens:
                open_bank(slot)
            z = sums[slot]
            for g in range(PASSES):
                nc.tensor.matmul_mx(
                    out=z[:],
                    lhsT=x_codes[:, b, g, :].bitcast(FP8X4),
                    lhsT_scale=x_scales[:, b, g, :],
                    rhs=wx_words[:, half, PASSES * gate + g, :].bitcast(FP4X4),
                    rhs_scale=wx_scales[:, PASSES * gate + g, N_TILE * half : N_TILE * (half + 1)],
                    start=(opens and g == 0),
                    stop=(not opens and g == PASSES - 1),
                )

        def multiply_h(slot, opens):
            half, gate, b = order[slot]
            chunk = chunk_of(half, gate)
            if opens:
                open_bank(slot)
            for g in range(PASSES):
                nc.tensor.matmul_mx(
                    out=sums[slot][:],
                    lhsT=h_codes[:, b, g, :].bitcast(FP8X4),
                    lhsT_scale=h_scales[:, b, g, :],
                    rhs=uh_codes[chunk][:, g, :].bitcast(FP8X4),
                    rhs_scale=uh_scales[chunk][:, g, :],
                    start=(opens and g == 0),
                    stop=(not opens and g == PASSES - 1),
                )

        def add_bias(slot):
            half, gate, b = order[slot]
            first = FEATURES * gate + N_TILE * half
            value = gates.tile([P, N_TILE], F32, tag="gate%d" % gate)
            for part in pieces(half, b):
                nc.vector.tensor_tensor(
                    out=value[:, part], in0=sums[slot][:, part], in1=bias[:, first + part.start : first + part.stop], op=ALU.add
                )
            live[(gate, half, b)] = value

        def squash(slot):
            half, gate, b = order[slot]
            value = live[(gate, half, b)]
            for part in pieces(half, b):
                nc.scalar.activation(out=value[:, part], in_=value[:, part], func=ACT.Tanh if gate == GATE_G else ACT.Sigmoid)

        def epilogue(what, half, b):
            last_tile = (half, b) == (order[-1][0], order[-1][2])
            tile_by_tile = len(HALF_GROUPS[half]) > 1
            if what == "tanh":
                live[("tanh", half, b)] = gates.tile([P, N_TILE], F32, tag="tanh", name="squashed")
            for part in pieces(half, b):
                cols = slice(N_TILE * half + part.start, N_TILE * half + part.stop)
                if what == "ig":
                    g_t = live[(GATE_G, half, b)][:, part]
                    (nc.vector if tile_by_tile else nc.gpsimd).tensor_tensor(out=g_t, in0=g_t, in1=live[(GATE_I, half, b)][:, part], op=ALU.mult)
                if what == "fc":
                    f_t = live[(GATE_F, half, b)][:, part]
                    (nc.vector if tile_by_tile else nc.gpsimd).tensor_tensor(out=f_t, in0=f_t, in1=c_old[:, b, cols], op=ALU.mult)
                if what == "cell":
                    f_t = live[(GATE_F, half, b)][:, part]
                    adder = nc.gpsimd if tile_by_tile and not last_tile else nc.vector
                    adder.tensor_tensor(out=f_t, in0=f_t, in1=live[(GATE_G, half, b)][:, part], op=ALU.add)
                    nc.sync.dma_start(out=by_tile(out_1)[:, b, cols], in_=f_t)
                if what == "tanh":
                    nc.scalar.activation(out=live[("tanh", half, b)][:, part], in_=live[(GATE_F, half, b)][:, part], func=ACT.Tanh)
                if what == "out":
                    o_t = live[(GATE_O, half, b)][:, part]
                    (nc.gpsimd if (b < BATCH_TILES - 2 if tile_by_tile else 3 <= b < 5) else nc.vector).tensor_tensor(out=o_t, in0=o_t, in1=live[("tanh", half, b)][:, part], op=ALU.mult)
                    nc.sync.dma_start(out=by_tile(out_0)[:, b, cols], in_=o_t)

        transpose_uh(0)
        nc.sync.dma_start(out=c_old[:], in_=by_tile(c_pre))
        load_uh(UH_RAW_BUFS)
        spread_bias(1, nc.vector.tensor_copy)
        quantise_uh(0)
        for early in range(EARLY_X // 2):
            multiply_x(early, True)
        quantise_activations(h_raw, False, nc.scalar.copy, h_codes, h_scales)
        for early in range(EARLY_X // 2, EARLY_X):
            multiply_x(early, True)
        x_was_last = [True]

        for slot in range(STEPS + DRAIN):
            if slot < STEPS:
                run = TILE_RUN if len(HALF_GROUPS[order[slot][0]]) > 1 else RUN
                if slot % run == 0:
                    if slot in transposed_before:
                        transpose_uh(transposed_before[slot])
                        behind = transposed_before[slot] + UH_RAW_BUFS
                        if behind < CHUNKS:
                            load_uh(behind)
                        if behind - 1 < CHUNKS:
                            load_wx_words(gate_of(behind - 1), 1)
                    members = range(slot, min(slot + run, STEPS))
                    if slot < EARLY_X:
                        for member in members:
                            multiply_h(member, False)
                        x_was_last[0] = False
                    elif x_was_last[0] or not ALTERNATE:
                        for member in members:
                            multiply_x(member, True)
                        for member in members:
                            multiply_h(member, False)
                        x_was_last[0] = False
                    else:
                        for member in members:
                            multiply_h(member, True)
                        for member in members:
                            multiply_x(member, False)
                        x_was_last[0] = True
                add_bias(slot)
                if slot - QUANT_LAG in transposed_before:
                    quantise_uh(transposed_before[slot - QUANT_LAG])
            for what, (half, b) in due.get(slot, []):
                if what == "tanh" and len(HALF_GROUPS[half]) == 1:
                    epilogue(what, half, b)
            if slot < STEPS:
                squash(slot)
            for kind in ("tanh", "ig", "fc", "cell", "out"):
                for what, (half, b) in due.get(slot, []):
                    if what == kind and not (what == "tanh" and len(HALF_GROUPS[half]) == 1):
                        epilogue(what, half, b)
